import numpy as np
import ml_dtypes


def mxq(x, axis, fmt="e4m3"):
    dtype, down = {"e4m3": (ml_dtypes.float8_e4m3fn, 7), "e5m2": (ml_dtypes.float8_e5m2, 14)}[fmt]
    v = np.moveaxis(np.asarray(x, np.float32).astype(ml_dtypes.bfloat16).astype(np.float64), axis, -1)
    blocks = v.reshape(v.shape[:-1] + (-1, 32))
    amax = np.abs(blocks).max(-1, keepdims=True)
    byte = np.maximum(np.where(amax > 0, np.frexp(amax)[1] - 1 + 127, 0) - down, 1)
    scale = np.exp2(byte - 127.0)
    codes = (blocks / scale).astype(np.float32).astype(dtype).astype(np.float64)
    return np.moveaxis((codes * scale).reshape(v.shape), -1, axis)


WIDE = False


def mx_kscale(k):
    if not WIDE:
        return np.ones(k)
    levels = np.array([10, -10, 5, -5, 0])
    if k % 512:
        return np.exp2(np.random.permutation(np.resize(levels, k // 32))).repeat(32)
    a = np.empty((k // 512, 16))
    for p in range(k // 512):
        a[p, :8] = np.random.permutation(np.resize(levels, 8))
        for g in range(8):
            far = levels[np.abs(levels - a[p, g]) >= 10]
            a[p, g + 8] = far[np.random.randint(len(far))]
    return np.exp2(a.ravel()).repeat(32)


BF16 = ml_dtypes.bfloat16


def bf(x):
    return np.asarray(x, np.float32).astype(BF16)


def f64(x):
    return np.asarray(x).astype(np.float64)


B, In, H, Hh, E, G = 4096, 256, 256, 128, 128, 4
K = In + H
EPS = 1e-6


def rn(*shape):
    return np.random.standard_normal(shape)


def sigmoid(v):
    return 1.0 / (1.0 + np.exp(-v))


def ln(a, gamma, beta):
    mean = a.mean(-1, keepdims=True)
    std = a.std(-1, keepdims=True, ddof=1)
    return gamma * (a - mean) / (std + EPS) + beta


def setup_inputs():
    s = mx_kscale(K)
    return {
        'x': bf(rn(B, In) * s[:In]),
        'h': bf(rn(B, H) * s[In:]),
        'hyper_h': bf(rn(B, Hh)),
        'hyper_c': bf(rn(B, Hh)),
        'hc_Wih': bf(rn(G * Hh, K) / np.sqrt(K) / s[None, :]),
        'hc_bih': bf(0.3 * rn(G * Hh)),
        'hc_Whh': bf(rn(G * Hh, Hh) / np.sqrt(Hh)),
        'hc_ln_gamma': bf(1.0 + 0.1 * rn(G, Hh)),
        'hc_ln_beta': bf(0.1 * rn(G, Hh)),
        'hc_lnc_gamma': bf(1.0 + 0.1 * rn(Hh)),
        'hc_lnc_beta': bf(0.1 * rn(Hh)),
    }


def reference(x, h, hyper_h, hyper_c, hc_Wih, hc_bih, hc_Whh, hc_ln_gamma, hc_ln_beta, hc_lnc_gamma, hc_lnc_beta):
    hyper_in = np.concatenate([f64(x), f64(h)], axis=1)
    v = (mxq(hyper_in, 1, 'e4m3') @ mxq(f64(hc_Wih).T, 0, 'e4m3')) + f64(hc_bih) + f64(hyper_h) @ f64(hc_Whh).T
    v = ln(v.reshape(B, G, Hh), f64(hc_ln_gamma), f64(hc_ln_beta))
    hi, hf, hg, ho = v[:, 0], v[:, 1], v[:, 2], v[:, 3]
    hf = hf + 1.0
    new_hyper_c = f64(hyper_c) * sigmoid(hf) + sigmoid(hi) * np.tanh(hg)
    new_hyper_c = ln(new_hyper_c, f64(hc_lnc_gamma), f64(hc_lnc_beta))
    new_hyper_h = np.tanh(new_hyper_c) * sigmoid(ho)
    return new_hyper_h, new_hyper_c

@@ -1,0 +1,585 @@
+from contextlib import ExitStack
+
+import concourse.mybir as mybir
+from concourse.masks import make_identity
+
+F32 = mybir.dt.float32
+BF16 = mybir.dt.bfloat16
+U32 = mybir.dt.uint32
+U8 = mybir.dt.uint8
+FP8X4 = mybir.dt.float8_e4m3fn_x4
+ALU = mybir.AluOpType
+ACT = mybir.ActivationFunctionType
+
+P = 128
+BATCH = 4096
+IN = 256
+K = 2 * IN
+UNITS = 128
+GATES = 4
+EPS = 1e-6
+
+N_TILES = BATCH // P
+TILES_PER_GROUP = 2
+N_GROUPS = N_TILES // TILES_PER_GROUP
+GROUP_COLS = TILES_PER_GROUP * P
+GROUP_STATS = TILES_PER_GROUP * GATES
+WORDS = K // 2
+
+GATE_FUNCS = (ACT.Sigmoid, ACT.Sigmoid, ACT.Tanh, ACT.Sigmoid)
+FORGET = 1
+OUTPUT = 3
+
+CELL_LAG = 3
+ROUND_STATS = GROUP_STATS + TILES_PER_GROUP
+
+SCALAR_GATES = 2
+
+LOADS_AHEAD = 4
+
+FLOPS = 2 * BATCH * K * GATES * UNITS + 2 * BATCH * UNITS * GATES * UNITS
+
+
+def transpose_words(nc, psum, ident_f32, words):
+    k_first = psum.tile([P, 2, 2, P], F32, tag="in")
+    for i in range(2):
+        for u in range(2):
+            nc.tensor.transpose(k_first[:, i, u, :], words[i][:, u::2], ident_f32)
+    return k_first
+
+
+def group_words(nc, k_first, grouped):
+    nc.scalar.copy(
+        out=grouped.bitcast(F32).rearrange("p (i r u) -> p i r u", i=2, u=2),
+        in_=k_first[:].rearrange("p i u r -> p i r u"),
+    )
+
+
+def tile_hyperlstmcell_pa_t_kernel(
+    tc,
+    x,
+    h,
+    hyper_h,
+    hyper_c,
+    hc_Wih,
+    hc_bih,
+    hc_Whh,
+    hc_ln_gamma,
+    hc_ln_beta,
+    hc_lnc_gamma,
+    hc_lnc_beta,
+    out_0,
+    out_1,
+):
+    nc = tc.nc
+    with ExitStack() as ctx:
+        const = ctx.enter_context(tc.tile_pool(name="const", bufs=1))
+        work = ctx.enter_context(tc.tile_pool(name="work", bufs=2))
+        psum_in = ctx.enter_context(tc.psum_pool(name="psum_in", bufs=2))
+        psum_mx = ctx.enter_context(tc.psum_pool(name="psum_mx", bufs=2))
+        psum = ctx.enter_context(tc.psum_pool(name="psum", bufs=1))
+
+        x_rows = x.rearrange("(p r) k -> p (r k)", r=N_TILES)
+        h_rows = h.rearrange("(p r) k -> p (r k)", r=N_TILES)
+        hyper_h_rows = hyper_h.rearrange("(p r) k -> p (r k)", r=N_TILES)
+        hyper_c_rows = hyper_c.rearrange("(p r) k -> p (r k)", r=N_TILES)
+        new_h_rows = out_0.rearrange("(p r) k -> p (r k)", r=N_TILES)
+        new_c_rows = out_1.rearrange("(p r) k -> p (r k)", r=N_TILES)
+
+        kept_tiles = [dict() for group in range(N_GROUPS)]
+        shared_tiles = [dict() for r in range(N_GROUPS + CELL_LAG)]
+
+        def outside(group):
+            return group < 0 or group >= N_GROUPS
+
+        def live_columns(r):
+            first = 0 if r < N_GROUPS else GROUP_STATS
+            last = ROUND_STATS if r >= CELL_LAG else GROUP_STATS
+            return slice(first, last)
+
+        def load(group):
+            if outside(group):
+                return
+            u_sb = work.tile([P, TILES_PER_GROUP * K], BF16, bufs=LOADS_AHEAD)
+            u_parts = u_sb[:].rearrange("p (t s k) -> p t s k", t=TILES_PER_GROUP, s=2)
+            hyper_h_sb = work.tile([P, GROUP_COLS], BF16, bufs=LOADS_AHEAD)
+            hyper_c_sb = work.tile([P, GROUP_COLS], BF16, bufs=LOADS_AHEAD)
+            wide = slice(group * TILES_PER_GROUP * IN, (group + 1) * TILES_PER_GROUP * IN)
+            narrow = slice(group * GROUP_COLS, (group + 1) * GROUP_COLS)
+            nc.sync.dma_start(out=u_parts[:, :, 0, :], in_=x_rows[:, wide].rearrange("p (t k) -> p t k", t=TILES_PER_GROUP))
+            nc.sync.dma_start(out=u_parts[:, :, 1, :], in_=h_rows[:, wide].rearrange("p (t k) -> p t k", t=TILES_PER_GROUP))
+            nc.sync.dma_start(out=hyper_h_sb[:], in_=hyper_h_rows[:, narrow])
+            nc.sync.dma_start(out=hyper_c_sb[:], in_=hyper_c_rows[:, narrow])
+            kept_tiles[group]["u_sb"] = u_sb
+            kept_tiles[group]["hyper_h_sb"] = hyper_h_sb
+            kept_tiles[group]["hyper_c_sb"] = hyper_c_sb
+
+        wih_rows = const.tile([P, GATES * K], BF16)
+        nc.sync.dma_start(
+            out=wih_rows[:].rearrange("p (g k) -> p g k", g=GATES),
+            in_=hc_Wih.rearrange("(g p) k -> p g k", p=P),
+        )
+        load(0)
+        load(1)
+
+        ident_f32 = const.tile([P, P], F32)
+        make_identity(nc, ident_f32[:])
+        ident_bf16 = const.tile([P, P], BF16)
+        make_identity(nc, ident_bf16[:])
+
+        wih_words = wih_rows[:].bitcast(F32)
+        wih_grouped = const.tile([P, GATES * P * 4], BF16, align_bytes=64)
+        wih_codes = const.tile([P, GATES * P], U32, align_bytes=64)
+        wih_scales = const.tile([P, GATES * P], U8, align_bytes=64)
+        for pair in range(GATES // 2):
+            wih_t_ps = transpose_words(
+                nc,
+                psum_in,
+                ident_f32[:],
+                [wih_words[:, g * WORDS : (g + 1) * WORDS] for g in (2 * pair, 2 * pair + 1)],
+            )
+            group_words(nc, wih_t_ps, wih_grouped[:, 2 * pair * P * 4 : (2 * pair + 2) * P * 4])
+        nc.vector.quantize_mx(out=wih_codes[:].bitcast(FP8X4), scales=wih_scales[:], in_=wih_grouped[:])
+
+        whh_rows = const.tile([P, GATES * UNITS], BF16)
+        nc.scalar.dma_start(
+            out=whh_rows[:].rearrange("p (g k) -> p g k", g=GATES),
+            in_=hc_Whh.rearrange("(g p) k -> p g k", p=P),
+        )
+        whh_t_ps = psum.tile([P, GATES * P], BF16, tag="norm_if")
+        for g in range(GATES):
+            nc.tensor.transpose(
+                whh_t_ps[:, g * P : (g + 1) * P], whh_rows[:, g * UNITS : (g + 1) * UNITS], ident_bf16[:]
+            )
+        whh_t = const.tile([P, GATES * P], BF16)
+        nc.vector.tensor_copy(out=whh_t[:], in_=whh_t_ps[:])
+
+        vector_rows = const.tile([P, (GATES + 2) * UNITS], BF16)
+        nc.vector.memset(vector_rows[:], 0.0)
+        nc.scalar.dma_start(out=vector_rows[0:1, 0 : GATES * UNITS], in_=hc_bih.rearrange("(o n) -> o n", o=1))
+        nc.scalar.dma_start(
+            out=vector_rows[0:1, GATES * UNITS : (GATES + 1) * UNITS], in_=hc_lnc_gamma.rearrange("(o n) -> o n", o=1)
+        )
+        nc.scalar.dma_start(
+            out=vector_rows[0:1, (GATES + 1) * UNITS : (GATES + 2) * UNITS], in_=hc_lnc_beta.rearrange("(o n) -> o n", o=1)
+        )
+        ones = const.tile([P, P], BF16)
+        nc.vector.memset(ones[:], 1.0)
+        bias_ps = psum.tile([P, GATES, UNITS], F32, tag="norm_go")
+        nc.tensor.matmul(
+            out=bias_ps[:].rearrange("p g j -> p (g j)"),
+            lhsT=ones[:],
+            rhs=vector_rows[:, 0 : GATES * UNITS],
+            start=True,
+            stop=True,
+        )
+        bias_all = const.tile([P, GATES, UNITS], BF16)
+        nc.vector.tensor_copy(out=bias_all[:], in_=bias_ps[:])
+        cell_ps = psum.tile([P, 2, UNITS], F32, tag="back")
+        nc.tensor.matmul(
+            out=cell_ps[:].rearrange("p c j -> p (c j)"),
+            lhsT=ones[:],
+            rhs=vector_rows[:, GATES * UNITS : (GATES + 2) * UNITS],
+            start=True,
+            stop=True,
+        )
+        cell_all = const.tile([P, 2, UNITS], BF16)
+        nc.vector.tensor_copy(out=cell_all[:], in_=cell_ps[:])
+        gamma_c_all = cell_all[:, 0, :]
+        beta_c_all = cell_all[:, 1, :]
+
+        gate_rows = const.tile([P, P], BF16)
+        nc.vector.memset(gate_rows[:], 0.0)
+        nc.scalar.dma_start(out=gate_rows[0:GATES, :], in_=hc_ln_gamma)
+        nc.scalar.dma_start(out=gate_rows[GATES : 2 * GATES, :], in_=hc_ln_beta)
+        gate_cols_ps = psum.tile([P, P], BF16, tag="back")
+        nc.tensor.transpose(gate_cols_ps[:], gate_rows[:], ident_bf16[:])
+        gate_cols = const.tile([P, 2 * GATES], F32)
+        nc.vector.tensor_copy(out=gate_cols[:], in_=gate_cols_ps[:, 0 : 2 * GATES])
+        forget_beta = gate_cols[:, GATES + FORGET : GATES + FORGET + 1]
+        nc.vector.tensor_scalar_add(out=forget_beta, in0=forget_beta, scalar1=1.0)
+
+        half = const.tile([P, ROUND_STATS], F32)
+        nc.vector.memset(half[:], 0.5)
+
+        squares = const.tile([P, TILES_PER_GROUP, GATES, UNITS], F32)
+
+        def transpose_inputs(group):
+            if outside(group):
+                return
+            kept = kept_tiles[group]
+            u_words = kept["u_sb"][:].bitcast(F32)
+            kept["u_t_ps"] = transpose_words(
+                nc,
+                psum_in,
+                ident_f32[:],
+                [u_words[:, t * WORDS : (t + 1) * WORDS] for t in range(TILES_PER_GROUP)],
+            )
+            state_t_ps = psum_in.tile([P, 2, GROUP_COLS], BF16, tag="in")
+            for t in range(TILES_PER_GROUP):
+                cols = slice(t * P, (t + 1) * P)
+                nc.tensor.transpose(state_t_ps[:, 0, cols], kept["hyper_h_sb"][:, cols], ident_bf16[:])
+                nc.tensor.transpose(state_t_ps[:, 1, cols], kept["hyper_c_sb"][:, cols], ident_bf16[:])
+            kept["state_t_ps"] = state_t_ps
+
+        def copy_inputs(group):
+            if outside(group):
+                return
+            kept = kept_tiles[group]
+            u_grouped = work.tile([P, GROUP_COLS * 4], BF16, align_bytes=64)
+            group_words(nc, kept["u_t_ps"], u_grouped[:])
+            state_t = work.tile([P, 2, GROUP_COLS], BF16, bufs=5)
+            nc.scalar.copy(out=state_t[:], in_=kept["state_t_ps"][:])
+            kept["u_grouped"] = u_grouped
+            kept["hyper_h_t"] = state_t[:, 0, :]
+            kept["hyper_c_t"] = state_t[:, 1, :]
+
+        def quantise(group):
+            if outside(group):
+                return
+            kept = kept_tiles[group]
+            u_codes = work.tile([P, GROUP_COLS], U32, align_bytes=64)
+            u_scales = work.tile([P, GROUP_COLS], U8, align_bytes=64)
+            nc.vector.quantize_mx(out=u_codes[:].bitcast(FP8X4), scales=u_scales[:], in_=kept["u_grouped"][:])
+            kept["u_codes"] = u_codes
+            kept["u_scales"] = u_scales
+
+        def mx_product(group, t):
+            if outside(group):
+                return
+            kept = kept_tiles[group]
+            cols = slice(t * P, (t + 1) * P)
+            mx = psum_mx.tile([P, GATES, UNITS], F32)
+            nc.tensor.matmul_mx(
+                out=mx[:].rearrange("p g j -> p (g j)"),
+                lhsT=kept["u_codes"][:, cols].bitcast(FP8X4),
+                lhsT_scale=kept["u_scales"][:, cols],
+                rhs=wih_codes[:].bitcast(FP8X4),
+                rhs_scale=wih_scales[:],
+                start=True,
+                stop=True,
+            )
+            kept["mx", t] = mx
+
+        def plain_product(group, t):
+            if outside(group):
+                return
+            kept = kept_tiles[group]
+            plain = psum.tile([P, GATES, UNITS], F32, tag="plain")
+            nc.tensor.matmul(
+                out=plain[:].rearrange("p g j -> p (g j)"),
+                lhsT=kept["hyper_h_t"][:, t * P : (t + 1) * P],
+                rhs=whh_t[:],
+                start=True,
+                stop=True,
+            )
+            kept["plain", t] = plain
+
+        def add_bias(group, t):
+            if outside(group):
+                return
+            kept = kept_tiles[group]
+            plain_bias = work.tile([P, GATES, UNITS], F32)
+            nc.vector.tensor_tensor(out=plain_bias[:], in0=kept["plain", t][:], in1=bias_all[:], op=ALU.add)
+            kept["plain_bias", t] = plain_bias
+
+        def add_products(group, t):
+            if outside(group):
+                return
+            kept = kept_tiles[group]
+            if t == 0:
+                v = work.tile([P, TILES_PER_GROUP, GATES, UNITS], F32, bufs=3)
+                v_sum = work.tile([P, GROUP_STATS], F32, bufs=3)
+                kept["v"] = v
+                kept["v_sum"] = v_sum
+            for g in range(GATES):
+                nc.vector.scalar_tensor_tensor(
+                    out=kept["v"][:, t, g, :],
+                    in0=kept["mx", t][:, g, :],
+                    scalar=1.0,
+                    in1=kept["plain_bias", t][:, g, :],
+                    op0=ALU.mult,
+                    op1=ALU.add,
+                    accum_out=kept["v_sum"][:, t * GATES + g : t * GATES + g + 1],
+                )
+
+        def new_moments(r):
+            if r < 0 or r >= N_GROUPS + CELL_LAG:
+                return
+            moments = work.tile([P, 2 * GROUP_STATS], F32)
+            shared_tiles[r]["moments"] = moments
+
+        def sum_squares(group, t):
+            if outside(group):
+                return
+            kept = kept_tiles[group]
+            for g in range(GATES):
+                col = slice(t * GATES + g, t * GATES + g + 1)
+                nc.scalar.activation(
+                    out=squares[:, t, g, :],
+                    in_=kept["v"][:, t, g, :],
+                    func=ACT.Square,
+                    bias=kept["v_sum"][:, col],
+                    scale=-float(UNITS),
+                    accum_out=shared_tiles[group]["moments"][:, col],
+                )
+
+        def roots(r):
+            if r < 0 or r >= N_GROUPS + CELL_LAG:
+                return
+            shared = shared_tiles[r]
+            cols = live_columns(r)
+            root = work.tile([P, ROUND_STATS], F32)
+            nc.gpsimd.tensor_tensor(out=root[:, cols], in0=shared["moments"][:, cols], in1=half[:, cols], op=ALU.pow)
+            shared["root"] = root
+
+        def std_eps(r):
+            if r < 0 or r >= N_GROUPS + CELL_LAG:
+                return
+            shared = shared_tiles[r]
+            cols = live_columns(r)
+            std = work.tile([P, ROUND_STATS], F32)
+            nc.vector.tensor_scalar(
+                out=std[:, cols],
+                in0=shared["root"][:, cols],
+                scalar1=1.0 / (UNITS * (UNITS - 1) ** 0.5),
+                scalar2=EPS,
+                op0=ALU.mult,
+                op1=ALU.add,
+            )
+            shared["std"] = std
+
+        def inv_std(r):
+            if r < 0 or r >= N_GROUPS + CELL_LAG:
+                return
+            shared = shared_tiles[r]
+            cols = live_columns(r)
+            inv = work.tile([P, ROUND_STATS], F32)
+            nc.vector.reciprocal(out=inv[:, cols], in_=shared["std"][:, cols])
+            shared["inv"] = inv
+
+        def gate_shift(group):
+            if outside(group):
+                return
+            kept = kept_tiles[group]
+            shift = work.tile([P, GROUP_STATS], F32)
+            nc.vector.scalar_tensor_tensor(
+                out=shift[:],
+                in0=kept["v_sum"][:],
+                scalar=-1.0 / UNITS,
+                in1=shared_tiles[group]["inv"][:, 0:GROUP_STATS],
+                op0=ALU.mult,
+                op1=ALU.mult,
+            )
+            kept["shift"] = shift
+
+        def normalise_on_scalar(group):
+            if outside(group):
+                return
+            kept = kept_tiles[group]
+            normed = work.tile([P, TILES_PER_GROUP, GATES, UNITS], F32)
+            for g in range(SCALAR_GATES):
+                for t in range(TILES_PER_GROUP):
+                    col = slice(t * GATES + g, t * GATES + g + 1)
+                    nc.scalar.activation(
+                        out=normed[:, t, g, :],
+                        in_=kept["v"][:, t, g, :],
+                        func=ACT.Identity,
+                        scale=shared_tiles[group]["inv"][:, col],
+                        bias=kept["shift"][:, col],
+                    )
+            kept["normed"] = normed
+
+        def normalise_on_vector(group):
+            if outside(group):
+                return
+            kept = kept_tiles[group]
+            for g in range(SCALAR_GATES, GATES):
+                for t in range(TILES_PER_GROUP):
+                    col = slice(t * GATES + g, t * GATES + g + 1)
+                    nc.vector.tensor_scalar(
+                        out=kept["normed"][:, t, g, :],
+                        in0=kept["v"][:, t, g, :],
+                        scalar1=shared_tiles[group]["inv"][:, col],
+                        scalar2=kept["shift"][:, col],
+                        op0=ALU.mult,
+                        op1=ALU.add,
+                    )
+
+        def transpose_normed(group):
+            if outside(group):
+                return
+            kept = kept_tiles[group]
+            norm_if = psum.tile([P, 2, TILES_PER_GROUP, P], F32, tag="norm_if")
+            norm_go = psum.tile([P, 2, TILES_PER_GROUP, P], F32, tag="norm_go")
+            banks = (norm_if, norm_go)
+            for g in range(GATES):
+                for t in range(TILES_PER_GROUP):
+                    nc.tensor.transpose(banks[g // 2][:, g % 2, t, :], kept["normed"][:, t, g, :], ident_f32[:])
+            kept["banks"] = banks
+
+        def activate(group):
+            if outside(group):
+                return
+            kept = kept_tiles[group]
+            banks = kept["banks"]
+            gate_i = work.tile([P, GROUP_COLS], F32)
+            gate_f = work.tile([P, GROUP_COLS], F32)
+            gate_g = work.tile([P, GROUP_COLS], F32)
+            gate_o = work.tile([P, GROUP_COLS], F32, bufs=5)
+            gates = (gate_i, gate_f, gate_g, gate_o)
+            for g in range(GATES):
+                nc.scalar.activation(
+                    out=gates[g][:],
+                    in_=banks[g // 2][:, g % 2, :, :].rearrange("p t b -> p (t b)"),
+                    func=GATE_FUNCS[g],
+                    scale=gate_cols[:, g : g + 1],
+                    bias=gate_cols[:, GATES + g : GATES + g + 1],
+                )
+            kept["gates"] = gates
+
+        def cell_parts(group):
+            if outside(group):
+                return
+            kept = kept_tiles[group]
+            gate_i, gate_f, gate_g, gate_o = kept["gates"]
+            old_part = work.tile([P, GROUP_COLS], F32)
+            nc.gpsimd.tensor_tensor(out=old_part[:], in0=gate_f[:], in1=kept["hyper_c_t"], op=ALU.mult)
+            new_part = work.tile([P, GROUP_COLS], F32)
+            nc.gpsimd.tensor_tensor(out=new_part[:], in0=gate_i[:], in1=gate_g[:], op=ALU.mult)
+            kept["old_part"] = old_part
+            kept["new_part"] = new_part
+
+        def cell_sum(group):
+            if outside(group):
+                return
+            kept = kept_tiles[group]
+            raw_c = work.tile([P, GROUP_COLS], F32)
+            nc.vector.tensor_tensor(out=raw_c[:], in0=kept["old_part"][:], in1=kept["new_part"][:], op=ALU.add)
+            kept["raw_c"] = raw_c
+
+        def transpose_back(cell_group, gate_group):
+            if outside(cell_group) and outside(gate_group):
+                return
+            back = psum.tile([P, 2, TILES_PER_GROUP, UNITS], F32, tag="back")
+            for t in range(TILES_PER_GROUP):
+                cols = slice(t * P, (t + 1) * P)
+                if not outside(cell_group):
+                    nc.tensor.transpose(back[:, 0, t, :], kept_tiles[cell_group]["raw_c"][:, cols], ident_f32[:])
+                if not outside(gate_group):
+                    nc.tensor.transpose(back[:, 1, t, :], kept_tiles[gate_group]["gates"][OUTPUT][:, cols], ident_f32[:])
+            if not outside(cell_group):
+                kept_tiles[cell_group]["raw_c_rows"] = back[:, 0, :, :]
+            if not outside(gate_group):
+                kept_tiles[gate_group]["gate_o_rows"] = back[:, 1, :, :]
+
+        def cell_moments(group):
+            if outside(group):
+                return
+            kept = kept_tiles[group]
+            c_stats = work.tile([P, TILES_PER_GROUP, 6], F32)
+            for t in range(TILES_PER_GROUP):
+                nc.vector.bn_stats(out=c_stats[:, t, :], in_=kept["raw_c_rows"][:, t, :])
+            kept["c_stats"] = c_stats
+
+        def cell_centre(group):
+            if outside(group):
+                return
+            kept = kept_tiles[group]
+            c_mean_var = work.tile([P, TILES_PER_GROUP, 2], F32)
+            for t in range(TILES_PER_GROUP):
+                nc.vector.bn_aggr(out=c_mean_var[:, t, :], in_=kept["c_stats"][:, t, :])
+            centred = work.tile([P, TILES_PER_GROUP, UNITS], F32, bufs=3)
+            for t in range(TILES_PER_GROUP):
+                nc.vector.scalar_tensor_tensor(
+                    out=centred[:, t, :],
+                    in0=kept["raw_c_rows"][:, t, :],
+                    scalar=c_mean_var[:, t, 0:1],
+                    in1=gamma_c_all,
+                    op0=ALU.subtract,
+                    op1=ALU.mult,
+                )
+            kept["c_mean_var"] = c_mean_var
+            kept["centred"] = centred
+
+        def cell_variance(group):
+            if outside(group):
+                return
+            nc.vector.tensor_scalar_mul(
+                out=shared_tiles[group + CELL_LAG]["moments"][:, GROUP_STATS:ROUND_STATS],
+                in0=kept_tiles[group]["c_mean_var"][:, :, 1],
+                scalar1=float(UNITS**3),
+            )
+
+        def cell_out(group):
+            if outside(group):
+                return
+            kept = kept_tiles[group]
+            new_c = work.tile([P, TILES_PER_GROUP, UNITS], F32, bufs=3)
+            for t in range(TILES_PER_GROUP):
+                nc.vector.scalar_tensor_tensor(
+                    out=new_c[:, t, :],
+                    in0=kept["centred"][:, t, :],
+                    scalar=shared_tiles[group + CELL_LAG]["inv"][:, GROUP_STATS + t : GROUP_STATS + t + 1],
+                    in1=beta_c_all,
+                    op0=ALU.mult,
+                    op1=ALU.add,
+                )
+            kept["new_c"] = new_c[:].rearrange("p t j -> p (t j)")
+            nc.sync.dma_start(out=new_c_rows[:, group * GROUP_COLS : (group + 1) * GROUP_COLS], in_=kept["new_c"])
+
+        def cell_tanh(group):
+            if outside(group):
+                return
+            kept = kept_tiles[group]
+            tanh_c = work.tile([P, GROUP_COLS], F32)
+            nc.scalar.activation(out=tanh_c[:], in_=kept["new_c"], func=ACT.Tanh)
+            kept["tanh_c"] = tanh_c
+
+        def hidden_out(group):
+            if outside(group):
+                return
+            kept = kept_tiles[group]
+            new_h = work.tile([P, GROUP_COLS], F32, bufs=3)
+            nc.vector.tensor_tensor(
+                out=new_h[:],
+                in0=kept["gate_o_rows"].rearrange("p t j -> p (t j)"),
+                in1=kept["tanh_c"][:],
+                op=ALU.mult,
+            )
+            nc.sync.dma_start(out=new_h_rows[:, group * GROUP_COLS : (group + 1) * GROUP_COLS], in_=new_h[:])
+
+        with tc.manual_schedule():
+            for i in range(-2, N_GROUPS + 6):
+                load(i + 4)
+                new_moments(i)
+                activate(i - 2)
+                add_bias(i, 0)
+                plain_product(i, 1)
+                cell_parts(i - 2)
+                cell_moments(i - 3)
+                hidden_out(i - 6)
+                cell_tanh(i - 5)
+                transpose_inputs(i + 2)
+                add_products(i, 0)
+                copy_inputs(i + 2)
+                mx_product(i + 1, 0)
+                add_bias(i, 1)
+                plain_product(i + 1, 0)
+                cell_centre(i - 3)
+                sum_squares(i, 0)
+                add_products(i, 1)
+                mx_product(i + 1, 1)
+                sum_squares(i, 1)
+                cell_variance(i - 3)
+                roots(i)
+                std_eps(i - 1)
+                quantise(i + 2)
+                inv_std(i - 1)
+                cell_sum(i - 2)
+                transpose_back(i - 2, i - 5)
+                gate_shift(i - 1)
+                normalise_on_scalar(i - 1)
+                cell_out(i - 4)
+                normalise_on_vector(i - 1)
+                transpose_normed(i - 1)

@@ -20,22 +20,21 @@ GATES = 4
 EPS = 1e-6
 
 N_TILES = BATCH // P
-TILES_PER_GROUP = 2
-N_GROUPS = N_TILES // TILES_PER_GROUP
-GROUP_COLS = TILES_PER_GROUP * P
-GROUP_STATS = TILES_PER_GROUP * GATES
+TILES = 2
+N_GROUPS = N_TILES // TILES
+COLS = TILES * P
+GATE_STATS = TILES * GATES
 WORDS = K // 2
 
 GATE_FUNCS = (ACT.Sigmoid, ACT.Sigmoid, ACT.Tanh, ACT.Sigmoid)
-FORGET = 1
-OUTPUT = 3
+INPUT, FORGET, CELL, OUTPUT = range(GATES)
 
 CELL_LAG = 3
-ROUND_STATS = GROUP_STATS + TILES_PER_GROUP
+ROUND_STATS = GATE_STATS + TILES
 
-SCALAR_GATES = 2
+LOADS_AHEAD = 6
 
-LOADS_AHEAD = 4
+SCALAR_GATES = 3
 
 FLOPS = 2 * BATCH * K * GATES * UNITS + 2 * BATCH * UNITS * GATES * UNITS
 
@@ -75,9 +74,11 @@ def tile_hyperlstmcell_pa_t_kernel(
     with ExitStack() as ctx:
         const = ctx.enter_context(tc.tile_pool(name="const", bufs=1))
         work = ctx.enter_context(tc.tile_pool(name="work", bufs=2))
-        psum_in = ctx.enter_context(tc.psum_pool(name="psum_in", bufs=2))
-        psum_mx = ctx.enter_context(tc.psum_pool(name="psum_mx", bufs=2))
-        psum = ctx.enter_context(tc.psum_pool(name="psum", bufs=1))
+        psum_in = ctx.enter_context(tc.psum_pool(name="psum_in", bufs=1))
+        psum_mx = ctx.enter_context(tc.psum_pool(name="psum_mx", bufs=1))
+        psum_v = ctx.enter_context(tc.psum_pool(name="psum_v", bufs=4))
+        psum_norm = ctx.enter_context(tc.psum_pool(name="psum_norm", bufs=1))
+        psum_back = ctx.enter_context(tc.psum_pool(name="psum_back", bufs=1))
 
         x_rows = x.rearrange("(p r) k -> p (r k)", r=N_TILES)
         h_rows = h.rearrange("(p r) k -> p (r k)", r=N_TILES)
@@ -92,27 +93,31 @@ def tile_hyperlstmcell_pa_t_kernel(
         def outside(group):
             return group < 0 or group >= N_GROUPS
 
-        def live_columns(r):
-            first = 0 if r < N_GROUPS else GROUP_STATS
-            last = ROUND_STATS if r >= CELL_LAG else GROUP_STATS
+        def no_round(r):
+            return r < 0 or r >= N_GROUPS + CELL_LAG
+
+        def live(r):
+            first = 0 if r < N_GROUPS else GATE_STATS
+            last = ROUND_STATS if r >= CELL_LAG else GATE_STATS
             return slice(first, last)
 
         def load(group):
             if outside(group):
                 return
-            u_sb = work.tile([P, TILES_PER_GROUP * K], BF16, bufs=LOADS_AHEAD)
-            u_parts = u_sb[:].rearrange("p (t s k) -> p t s k", t=TILES_PER_GROUP, s=2)
-            hyper_h_sb = work.tile([P, GROUP_COLS], BF16, bufs=LOADS_AHEAD)
-            hyper_c_sb = work.tile([P, GROUP_COLS], BF16, bufs=LOADS_AHEAD)
-            wide = slice(group * TILES_PER_GROUP * IN, (group + 1) * TILES_PER_GROUP * IN)
-            narrow = slice(group * GROUP_COLS, (group + 1) * GROUP_COLS)
-            nc.sync.dma_start(out=u_parts[:, :, 0, :], in_=x_rows[:, wide].rearrange("p (t k) -> p t k", t=TILES_PER_GROUP))
-            nc.sync.dma_start(out=u_parts[:, :, 1, :], in_=h_rows[:, wide].rearrange("p (t k) -> p t k", t=TILES_PER_GROUP))
+            kept = kept_tiles[group]
+            u_sb = work.tile([P, TILES * K], BF16, bufs=LOADS_AHEAD)
+            hyper_h_sb = work.tile([P, COLS], BF16, bufs=LOADS_AHEAD)
+            hyper_c_sb = work.tile([P, COLS], BF16, bufs=LOADS_AHEAD + 4)
+            u_parts = u_sb[:].rearrange("p (t s k) -> p t s k", t=TILES, s=2)
+            wide = slice(group * TILES * IN, (group + 1) * TILES * IN)
+            narrow = slice(group * COLS, (group + 1) * COLS)
+            nc.sync.dma_start(out=u_parts[:, :, 0, :], in_=x_rows[:, wide].rearrange("p (t k) -> p t k", t=TILES))
+            nc.sync.dma_start(out=u_parts[:, :, 1, :], in_=h_rows[:, wide].rearrange("p (t k) -> p t k", t=TILES))
             nc.sync.dma_start(out=hyper_h_sb[:], in_=hyper_h_rows[:, narrow])
             nc.sync.dma_start(out=hyper_c_sb[:], in_=hyper_c_rows[:, narrow])
-            kept_tiles[group]["u_sb"] = u_sb
-            kept_tiles[group]["hyper_h_sb"] = hyper_h_sb
-            kept_tiles[group]["hyper_c_sb"] = hyper_c_sb
+            kept["u_sb"] = u_sb
+            kept["hyper_h_sb"] = hyper_h_sb
+            kept["hyper_c_sb"] = hyper_c_sb
 
         wih_rows = const.tile([P, GATES * K], BF16)
         nc.sync.dma_start(
@@ -125,7 +130,20 @@ def tile_hyperlstmcell_pa_t_kernel(
         ident_f32 = const.tile([P, P], F32)
         make_identity(nc, ident_f32[:])
         ident_bf16 = const.tile([P, P], BF16)
-        make_identity(nc, ident_bf16[:])
+        nc.vector.tensor_copy(out=ident_bf16[:], in_=ident_f32[:])
+
+        rows = const.tile([P, P], BF16)
+        nc.vector.memset(rows[:], 0.0)
+        nc.scalar.dma_start(out=rows[0:GATES, :], in_=hc_ln_gamma)
+        nc.scalar.dma_start(out=rows[GATES : 2 * GATES, :], in_=hc_ln_beta)
+        nc.scalar.dma_start(out=rows[2 * GATES : 3 * GATES, :], in_=hc_bih.rearrange("(g j) -> g j", g=GATES))
+        nc.scalar.dma_start(out=rows[3 * GATES : 3 * GATES + 1, :], in_=hc_lnc_gamma.rearrange("(o n) -> o n", o=1))
+        nc.scalar.dma_start(out=rows[3 * GATES + 1 : 3 * GATES + 2, :], in_=hc_lnc_beta.rearrange("(o n) -> o n", o=1))
+        whh_rows = const.tile([P, GATES * UNITS], BF16)
+        nc.scalar.dma_start(
+            out=whh_rows[:].rearrange("p (g k) -> p g k", g=GATES),
+            in_=hc_Whh.rearrange("(g p) k -> p g k", p=P),
+        )
 
         wih_words = wih_rows[:].bitcast(F32)
         wih_grouped = const.tile([P, GATES * P * 4], BF16, align_bytes=64)
@@ -133,20 +151,19 @@ def tile_hyperlstmcell_pa_t_kernel(
         wih_scales = const.tile([P, GATES * P], U8, align_bytes=64)
         for pair in range(GATES // 2):
             wih_t_ps = transpose_words(
-                nc,
-                psum_in,
-                ident_f32[:],
-                [wih_words[:, g * WORDS : (g + 1) * WORDS] for g in (2 * pair, 2 * pair + 1)],
+                nc, psum_in, ident_f32[:], [wih_words[:, g * WORDS : (g + 1) * WORDS] for g in (2 * pair, 2 * pair + 1)]
             )
             group_words(nc, wih_t_ps, wih_grouped[:, 2 * pair * P * 4 : (2 * pair + 2) * P * 4])
         nc.vector.quantize_mx(out=wih_codes[:].bitcast(FP8X4), scales=wih_scales[:], in_=wih_grouped[:])
 
-        whh_rows = const.tile([P, GATES * UNITS], BF16)
-        nc.scalar.dma_start(
-            out=whh_rows[:].rearrange("p (g k) -> p g k", g=GATES),
-            in_=hc_Whh.rearrange("(g p) k -> p g k", p=P),
-        )
-        whh_t_ps = psum.tile([P, GATES * P], BF16, tag="norm_if")
+        cols_ps = psum_v.tile([P, P], BF16, tag="v")
+        nc.tensor.transpose(cols_ps[:], rows[:], ident_bf16[:])
+        cols = const.tile([P, 3 * GATES + 2], F32)
+        nc.vector.tensor_copy(out=cols[:], in_=cols_ps[:, 0 : 3 * GATES + 2])
+        forget_beta = cols[:, GATES + FORGET : GATES + FORGET + 1]
+        nc.vector.tensor_scalar_add(out=forget_beta, in0=forget_beta, scalar1=1.0)
+
+        whh_t_ps = psum_v.tile([P, GATES * P], BF16, tag="v")
         for g in range(GATES):
             nc.tensor.transpose(
                 whh_t_ps[:, g * P : (g + 1) * P], whh_rows[:, g * UNITS : (g + 1) * UNITS], ident_bf16[:]
@@ -154,195 +171,158 @@ def tile_hyperlstmcell_pa_t_kernel(
         whh_t = const.tile([P, GATES * P], BF16)
         nc.vector.tensor_copy(out=whh_t[:], in_=whh_t_ps[:])
 
-        vector_rows = const.tile([P, (GATES + 2) * UNITS], BF16)
-        nc.vector.memset(vector_rows[:], 0.0)
-        nc.scalar.dma_start(out=vector_rows[0:1, 0 : GATES * UNITS], in_=hc_bih.rearrange("(o n) -> o n", o=1))
-        nc.scalar.dma_start(
-            out=vector_rows[0:1, GATES * UNITS : (GATES + 1) * UNITS], in_=hc_lnc_gamma.rearrange("(o n) -> o n", o=1)
-        )
-        nc.scalar.dma_start(
-            out=vector_rows[0:1, (GATES + 1) * UNITS : (GATES + 2) * UNITS], in_=hc_lnc_beta.rearrange("(o n) -> o n", o=1)
-        )
-        ones = const.tile([P, P], BF16)
-        nc.vector.memset(ones[:], 1.0)
-        bias_ps = psum.tile([P, GATES, UNITS], F32, tag="norm_go")
-        nc.tensor.matmul(
-            out=bias_ps[:].rearrange("p g j -> p (g j)"),
-            lhsT=ones[:],
-            rhs=vector_rows[:, 0 : GATES * UNITS],
-            start=True,
-            stop=True,
-        )
-        bias_all = const.tile([P, GATES, UNITS], BF16)
-        nc.vector.tensor_copy(out=bias_all[:], in_=bias_ps[:])
-        cell_ps = psum.tile([P, 2, UNITS], F32, tag="back")
-        nc.tensor.matmul(
-            out=cell_ps[:].rearrange("p c j -> p (c j)"),
-            lhsT=ones[:],
-            rhs=vector_rows[:, GATES * UNITS : (GATES + 2) * UNITS],
-            start=True,
-            stop=True,
-        )
-        cell_all = const.tile([P, 2, UNITS], BF16)
+        cell_ps = psum_v.tile([P, 2, UNITS], F32, tag="v")
+        for c in range(2):
+            col = cols[:, 3 * GATES + c : 3 * GATES + c + 1]
+            nc.tensor.transpose(cell_ps[:, c, :], col.to_broadcast([P, P]), ident_f32[:])
+        cell_all = const.tile([P, 2, UNITS], F32)
         nc.vector.tensor_copy(out=cell_all[:], in_=cell_ps[:])
         gamma_c_all = cell_all[:, 0, :]
         beta_c_all = cell_all[:, 1, :]
 
-        gate_rows = const.tile([P, P], BF16)
-        nc.vector.memset(gate_rows[:], 0.0)
-        nc.scalar.dma_start(out=gate_rows[0:GATES, :], in_=hc_ln_gamma)
-        nc.scalar.dma_start(out=gate_rows[GATES : 2 * GATES, :], in_=hc_ln_beta)
-        gate_cols_ps = psum.tile([P, P], BF16, tag="back")
-        nc.tensor.transpose(gate_cols_ps[:], gate_rows[:], ident_bf16[:])
-        gate_cols = const.tile([P, 2 * GATES], F32)
-        nc.vector.tensor_copy(out=gate_cols[:], in_=gate_cols_ps[:, 0 : 2 * GATES])
-        forget_beta = gate_cols[:, GATES + FORGET : GATES + FORGET + 1]
-        nc.vector.tensor_scalar_add(out=forget_beta, in0=forget_beta, scalar1=1.0)
-
         half = const.tile([P, ROUND_STATS], F32)
         nc.vector.memset(half[:], 0.5)
 
-        squares = const.tile([P, TILES_PER_GROUP, GATES, UNITS], F32)
-
-        def transpose_inputs(group):
+        def transpose_u(group):
             if outside(group):
                 return
             kept = kept_tiles[group]
             u_words = kept["u_sb"][:].bitcast(F32)
-            kept["u_t_ps"] = transpose_words(
-                nc,
-                psum_in,
-                ident_f32[:],
-                [u_words[:, t * WORDS : (t + 1) * WORDS] for t in range(TILES_PER_GROUP)],
+            kept["u_t"] = transpose_words(
+                nc, psum_in, ident_f32[:], [u_words[:, t * WORDS : (t + 1) * WORDS] for t in range(TILES)]
             )
-            state_t_ps = psum_in.tile([P, 2, GROUP_COLS], BF16, tag="in")
-            for t in range(TILES_PER_GROUP):
-                cols = slice(t * P, (t + 1) * P)
-                nc.tensor.transpose(state_t_ps[:, 0, cols], kept["hyper_h_sb"][:, cols], ident_bf16[:])
-                nc.tensor.transpose(state_t_ps[:, 1, cols], kept["hyper_c_sb"][:, cols], ident_bf16[:])
-            kept["state_t_ps"] = state_t_ps
 
-        def copy_inputs(group):
+        def copy_u(group):
             if outside(group):
                 return
             kept = kept_tiles[group]
-            u_grouped = work.tile([P, GROUP_COLS * 4], BF16, align_bytes=64)
-            group_words(nc, kept["u_t_ps"], u_grouped[:])
-            state_t = work.tile([P, 2, GROUP_COLS], BF16, bufs=5)
-            nc.scalar.copy(out=state_t[:], in_=kept["state_t_ps"][:])
+            u_grouped = work.tile([P, COLS * 4], BF16, align_bytes=64)
+            group_words(nc, kept["u_t"], u_grouped[:])
             kept["u_grouped"] = u_grouped
-            kept["hyper_h_t"] = state_t[:, 0, :]
-            kept["hyper_c_t"] = state_t[:, 1, :]
 
         def quantise(group):
             if outside(group):
                 return
             kept = kept_tiles[group]
-            u_codes = work.tile([P, GROUP_COLS], U32, align_bytes=64)
-            u_scales = work.tile([P, GROUP_COLS], U8, align_bytes=64)
+            u_codes = work.tile([P, COLS], U32, align_bytes=64)
+            u_scales = work.tile([P, COLS], U8, align_bytes=64)
             nc.vector.quantize_mx(out=u_codes[:].bitcast(FP8X4), scales=u_scales[:], in_=kept["u_grouped"][:])
             kept["u_codes"] = u_codes
             kept["u_scales"] = u_scales
 
-        def mx_product(group, t):
+        def mx_product(group, pair):
             if outside(group):
                 return
             kept = kept_tiles[group]
-            cols = slice(t * P, (t + 1) * P)
-            mx = psum_mx.tile([P, GATES, UNITS], F32)
-            nc.tensor.matmul_mx(
-                out=mx[:].rearrange("p g j -> p (g j)"),
-                lhsT=kept["u_codes"][:, cols].bitcast(FP8X4),
-                lhsT_scale=kept["u_scales"][:, cols],
-                rhs=wih_codes[:].bitcast(FP8X4),
-                rhs_scale=wih_scales[:],
-                start=True,
-                stop=True,
-            )
-            kept["mx", t] = mx
+            mx = psum_mx.tile([P, 2, COLS], F32)
+            for e in range(2):
+                g = 2 * pair + e
+                nc.tensor.matmul_mx(
+                    out=mx[:, e, :],
+                    lhsT=wih_codes[:, g * P : (g + 1) * P].bitcast(FP8X4),
+                    lhsT_scale=wih_scales[:, g * P : (g + 1) * P],
+                    rhs=kept["u_codes"][:].bitcast(FP8X4),
+                    rhs_scale=kept["u_scales"][:],
+                    start=True,
+                    stop=True,
+                )
+            kept["mx", pair] = mx
 
-        def plain_product(group, t):
+        def add_bias(group, pair):
             if outside(group):
                 return
             kept = kept_tiles[group]
-            plain = psum.tile([P, GATES, UNITS], F32, tag="plain")
+            if pair == 0:
+                mx_bias = work.tile([P, GATES, COLS], F32)
+                kept["mx_bias"] = mx_bias
+            for e in range(2):
+                g = 2 * pair + e
+                nc.scalar.activation(
+                    out=kept["mx_bias"][:, g, :],
+                    in_=kept["mx", pair][:, e, :],
+                    func=ACT.Identity,
+                    bias=cols[:, 2 * GATES + g : 2 * GATES + g + 1],
+                )
+
+        def transpose_states(early, late):
+            if outside(early) and outside(late):
+                return
+            states = psum_in.tile([P, 2, COLS], BF16, tag="in")
+            for t in range(TILES):
+                part = slice(t * P, (t + 1) * P)
+                if not outside(early):
+                    nc.tensor.transpose(states[:, 0, part], kept_tiles[early]["hyper_h_sb"][:, part], ident_bf16[:])
+            for t in range(TILES):
+                part = slice(t * P, (t + 1) * P)
+                if not outside(late):
+                    nc.tensor.transpose(states[:, 1, part], kept_tiles[late]["hyper_c_sb"][:, part], ident_bf16[:])
+            if not outside(early):
+                kept_tiles[early]["hyper_h_ps"] = states[:, 0, :]
+            if not outside(late):
+                kept_tiles[late]["hyper_c_ps"] = states[:, 1, :]
+
+        def copy_hyper_h(group):
+            if outside(group):
+                return
+            kept = kept_tiles[group]
+            hyper_h_t = work.tile([P, COLS], BF16)
+            nc.scalar.copy(out=hyper_h_t[:], in_=kept["hyper_h_ps"])
+            kept["hyper_h_t"] = hyper_h_t
+
+        def form_v(group, t):
+            if outside(group):
+                return
+            kept = kept_tiles[group]
+            v = psum_v.tile([P, GATES, UNITS], F32, tag="v")
             nc.tensor.matmul(
-                out=plain[:].rearrange("p g j -> p (g j)"),
+                out=v[:].rearrange("p g j -> p (g j)"),
                 lhsT=kept["hyper_h_t"][:, t * P : (t + 1) * P],
                 rhs=whh_t[:],
                 start=True,
-                stop=True,
+                stop=False,
             )
-            kept["plain", t] = plain
-
-        def add_bias(group, t):
-            if outside(group):
-                return
-            kept = kept_tiles[group]
-            plain_bias = work.tile([P, GATES, UNITS], F32)
-            nc.vector.tensor_tensor(out=plain_bias[:], in0=kept["plain", t][:], in1=bias_all[:], op=ALU.add)
-            kept["plain_bias", t] = plain_bias
-
-        def add_products(group, t):
-            if outside(group):
-                return
-            kept = kept_tiles[group]
-            if t == 0:
-                v = work.tile([P, TILES_PER_GROUP, GATES, UNITS], F32, bufs=3)
-                v_sum = work.tile([P, GROUP_STATS], F32, bufs=3)
-                kept["v"] = v
-                kept["v_sum"] = v_sum
             for g in range(GATES):
-                nc.vector.scalar_tensor_tensor(
-                    out=kept["v"][:, t, g, :],
-                    in0=kept["mx", t][:, g, :],
-                    scalar=1.0,
-                    in1=kept["plain_bias", t][:, g, :],
-                    op0=ALU.mult,
-                    op1=ALU.add,
-                    accum_out=kept["v_sum"][:, t * GATES + g : t * GATES + g + 1],
+                nc.tensor.matmul(
+                    out=v[:, g, :],
+                    lhsT=kept["mx_bias"][:, g, t * P : (t + 1) * P],
+                    rhs=ident_f32[:],
+                    start=False,
+                    stop=g == GATES - 1,
+                    is_transpose=True,
                 )
+            kept["v", t] = v
 
         def new_moments(r):
-            if r < 0 or r >= N_GROUPS + CELL_LAG:
+            if no_round(r):
                 return
-            moments = work.tile([P, 2 * GROUP_STATS], F32)
+            moments = work.tile([P, ROUND_STATS, 3], F32, bufs=4)
             shared_tiles[r]["moments"] = moments
 
-        def sum_squares(group, t):
+        def gate_moments(group, t):
             if outside(group):
                 return
-            kept = kept_tiles[group]
-            for g in range(GATES):
-                col = slice(t * GATES + g, t * GATES + g + 1)
-                nc.scalar.activation(
-                    out=squares[:, t, g, :],
-                    in_=kept["v"][:, t, g, :],
-                    func=ACT.Square,
-                    bias=kept["v_sum"][:, col],
-                    scale=-float(UNITS),
-                    accum_out=shared_tiles[group]["moments"][:, col],
+            moments = shared_tiles[group]["moments"]
+            for pair in range(GATES // 2):
+                first = t * GATES + 2 * pair
+                nc.vector.bn_stats(
+                    out=moments[:, first : first + 2, :].rearrange("p s m -> p (s m)"),
+                    in_=kept_tiles[group]["v", t][:, 2 * pair : 2 * pair + 2, :].rearrange("p g j -> p j g"),
                 )
 
         def roots(r):
-            if r < 0 or r >= N_GROUPS + CELL_LAG:
+            if no_round(r):
                 return
             shared = shared_tiles[r]
-            cols = live_columns(r)
+            live_cols = live(r)
             root = work.tile([P, ROUND_STATS], F32)
-            nc.gpsimd.tensor_tensor(out=root[:, cols], in0=shared["moments"][:, cols], in1=half[:, cols], op=ALU.pow)
-            shared["root"] = root
-
-        def std_eps(r):
-            if r < 0 or r >= N_GROUPS + CELL_LAG:
-                return
-            shared = shared_tiles[r]
-            cols = live_columns(r)
+            nc.gpsimd.tensor_tensor(
+                out=root[:, live_cols], in0=shared["moments"][:, live_cols, 2], in1=half[:, live_cols], op=ALU.pow
+            )
             std = work.tile([P, ROUND_STATS], F32)
-            nc.vector.tensor_scalar(
-                out=std[:, cols],
-                in0=shared["root"][:, cols],
-                scalar1=1.0 / (UNITS * (UNITS - 1) ** 0.5),
+            nc.gpsimd.tensor_scalar(
+                out=std[:, live_cols],
+                in0=root[:, live_cols],
+                scalar1=1.0 / (UNITS - 1) ** 0.5,
                 scalar2=EPS,
                 op0=ALU.mult,
                 op1=ALU.add,
@@ -350,189 +330,173 @@ def tile_hyperlstmcell_pa_t_kernel(
             shared["std"] = std
 
         def inv_std(r):
-            if r < 0 or r >= N_GROUPS + CELL_LAG:
+            if no_round(r):
                 return
             shared = shared_tiles[r]
-            cols = live_columns(r)
+            live_cols = live(r)
             inv = work.tile([P, ROUND_STATS], F32)
-            nc.vector.reciprocal(out=inv[:, cols], in_=shared["std"][:, cols])
+            nc.vector.reciprocal(out=inv[:, live_cols], in_=shared["std"][:, live_cols])
             shared["inv"] = inv
 
         def gate_shift(group):
             if outside(group):
                 return
-            kept = kept_tiles[group]
-            shift = work.tile([P, GROUP_STATS], F32)
+            shift = work.tile([P, SCALAR_GATES], F32)
             nc.vector.scalar_tensor_tensor(
                 out=shift[:],
-                in0=kept["v_sum"][:],
-                scalar=-1.0 / UNITS,
-                in1=shared_tiles[group]["inv"][:, 0:GROUP_STATS],
+                in0=shared_tiles[group]["moments"][:, 0:SCALAR_GATES, 1],
+                scalar=-1.0,
+                in1=shared_tiles[group]["inv"][:, 0:SCALAR_GATES],
                 op0=ALU.mult,
                 op1=ALU.mult,
             )
-            kept["shift"] = shift
+            kept_tiles[group]["shift"] = shift
 
         def normalise_on_scalar(group):
             if outside(group):
                 return
             kept = kept_tiles[group]
-            normed = work.tile([P, TILES_PER_GROUP, GATES, UNITS], F32)
+            normed = work.tile([P, TILES, GATES, UNITS], F32)
             for g in range(SCALAR_GATES):
-                for t in range(TILES_PER_GROUP):
-                    col = slice(t * GATES + g, t * GATES + g + 1)
-                    nc.scalar.activation(
-                        out=normed[:, t, g, :],
-                        in_=kept["v"][:, t, g, :],
-                        func=ACT.Identity,
-                        scale=shared_tiles[group]["inv"][:, col],
-                        bias=kept["shift"][:, col],
-                    )
+                nc.scalar.activation(
+                    out=normed[:, 0, g, :],
+                    in_=kept["v", 0][:, g, :],
+                    func=ACT.Identity,
+                    scale=shared_tiles[group]["inv"][:, g : g + 1],
+                    bias=kept["shift"][:, g : g + 1],
+                )
             kept["normed"] = normed
 
         def normalise_on_vector(group):
             if outside(group):
                 return
             kept = kept_tiles[group]
-            for g in range(SCALAR_GATES, GATES):
-                for t in range(TILES_PER_GROUP):
-                    col = slice(t * GATES + g, t * GATES + g + 1)
-                    nc.vector.tensor_scalar(
-                        out=kept["normed"][:, t, g, :],
-                        in0=kept["v"][:, t, g, :],
-                        scalar1=shared_tiles[group]["inv"][:, col],
-                        scalar2=kept["shift"][:, col],
-                        op0=ALU.mult,
-                        op1=ALU.add,
-                    )
-
-        def transpose_normed(group):
-            if outside(group):
-                return
-            kept = kept_tiles[group]
-            norm_if = psum.tile([P, 2, TILES_PER_GROUP, P], F32, tag="norm_if")
-            norm_go = psum.tile([P, 2, TILES_PER_GROUP, P], F32, tag="norm_go")
-            banks = (norm_if, norm_go)
-            for g in range(GATES):
-                for t in range(TILES_PER_GROUP):
-                    nc.tensor.transpose(banks[g // 2][:, g % 2, t, :], kept["normed"][:, t, g, :], ident_f32[:])
-            kept["banks"] = banks
-
-        def activate(group):
-            if outside(group):
-                return
-            kept = kept_tiles[group]
-            banks = kept["banks"]
-            gate_i = work.tile([P, GROUP_COLS], F32)
-            gate_f = work.tile([P, GROUP_COLS], F32)
-            gate_g = work.tile([P, GROUP_COLS], F32)
-            gate_o = work.tile([P, GROUP_COLS], F32, bufs=5)
-            gates = (gate_i, gate_f, gate_g, gate_o)
-            for g in range(GATES):
-                nc.scalar.activation(
-                    out=gates[g][:],
-                    in_=banks[g // 2][:, g % 2, :, :].rearrange("p t b -> p (t b)"),
-                    func=GATE_FUNCS[g],
-                    scale=gate_cols[:, g : g + 1],
-                    bias=gate_cols[:, GATES + g : GATES + g + 1],
+            for t, g in [(1, g) for g in range(GATES)] + [(0, g) for g in range(SCALAR_GATES, GATES)]:
+                s = t * GATES + g
+                nc.vector.tensor_scalar(
+                    out=kept["normed"][:, t, g, :],
+                    in0=kept["v", t][:, g, :],
+                    scalar1=shared_tiles[group]["moments"][:, s, 1:2],
+                    scalar2=shared_tiles[group]["inv"][:, s : s + 1],
+                    op0=ALU.subtract,
+                    op1=ALU.mult,
                 )
-            kept["gates"] = gates
 
-        def cell_parts(group):
+        def transpose_normed(group, pair):
             if outside(group):
                 return
             kept = kept_tiles[group]
-            gate_i, gate_f, gate_g, gate_o = kept["gates"]
-            old_part = work.tile([P, GROUP_COLS], F32)
-            nc.gpsimd.tensor_tensor(out=old_part[:], in0=gate_f[:], in1=kept["hyper_c_t"], op=ALU.mult)
-            new_part = work.tile([P, GROUP_COLS], F32)
-            nc.gpsimd.tensor_tensor(out=new_part[:], in0=gate_i[:], in1=gate_g[:], op=ALU.mult)
-            kept["old_part"] = old_part
-            kept["new_part"] = new_part
+            norm = psum_norm.tile([P, 2, TILES, P], F32)
+            for e in range(2):
+                for t in range(TILES):
+                    nc.tensor.transpose(norm[:, e, t, :], kept["normed"][:, t, 2 * pair + e, :], ident_f32[:])
+            kept["norm", pair] = norm
 
-        def cell_sum(group):
+        def activate(group, pair):
             if outside(group):
                 return
             kept = kept_tiles[group]
-            raw_c = work.tile([P, GROUP_COLS], F32)
-            nc.vector.tensor_tensor(out=raw_c[:], in0=kept["old_part"][:], in1=kept["new_part"][:], op=ALU.add)
-            kept["raw_c"] = raw_c
+            for e in range(2):
+                g = 2 * pair + e
+                gate = work.tile([P, COLS], F32, tag="gate_%d" % g, bufs=6 if g == OUTPUT else 3)
+                nc.scalar.activation(
+                    out=gate[:],
+                    in_=kept["norm", pair][:, e, :, :].rearrange("p t b -> p (t b)"),
+                    func=GATE_FUNCS[g],
+                    scale=cols[:, g : g + 1],
+                    bias=cols[:, GATES + g : GATES + g + 1],
+                )
+                kept["gate", g] = gate
+
+        def old_part(group):
+            if outside(group):
+                return
+            kept = kept_tiles[group]
+            old = work.tile([P, COLS], F32)
+            nc.vector.tensor_tensor(out=old[:], in0=kept["gate", FORGET][:], in1=kept["hyper_c_ps"], op=ALU.mult)
+            kept["old"] = old
+
+        def new_part(group):
+            if outside(group):
+                return
+            kept = kept_tiles[group]
+            new = work.tile([P, COLS], F32)
+            nc.gpsimd.tensor_tensor(out=new[:], in0=kept["gate", INPUT][:], in1=kept["gate", CELL][:], op=ALU.mult)
+            kept["new"] = new
 
         def transpose_back(cell_group, gate_group):
             if outside(cell_group) and outside(gate_group):
                 return
-            back = psum.tile([P, 2, TILES_PER_GROUP, UNITS], F32, tag="back")
-            for t in range(TILES_PER_GROUP):
-                cols = slice(t * P, (t + 1) * P)
-                if not outside(cell_group):
-                    nc.tensor.transpose(back[:, 0, t, :], kept_tiles[cell_group]["raw_c"][:, cols], ident_f32[:])
+            back = psum_back.tile([P, 2, TILES, UNITS], F32)
+            for t in range(TILES):
+                part = slice(t * P, (t + 1) * P)
                 if not outside(gate_group):
-                    nc.tensor.transpose(back[:, 1, t, :], kept_tiles[gate_group]["gates"][OUTPUT][:, cols], ident_f32[:])
+                    nc.tensor.transpose(back[:, 1, t, :], kept_tiles[gate_group]["gate", OUTPUT][:, part], ident_f32[:])
+            for t in range(TILES):
+                part = slice(t * P, (t + 1) * P)
+                if not outside(cell_group):
+                    kept = kept_tiles[cell_group]
+                    for source, first in ((kept["old"], True), (kept["new"], False)):
+                        nc.tensor.matmul(
+                            out=back[:, 0, t, :],
+                            lhsT=source[:, part],
+                            rhs=ident_f32[:],
+                            start=first,
+                            stop=not first,
+                            is_transpose=True,
+                        )
             if not outside(cell_group):
-                kept_tiles[cell_group]["raw_c_rows"] = back[:, 0, :, :]
+                kept_tiles[cell_group]["raw_c"] = back[:, 0, :, :]
             if not outside(gate_group):
                 kept_tiles[gate_group]["gate_o_rows"] = back[:, 1, :, :]
 
         def cell_moments(group):
             if outside(group):
                 return
-            kept = kept_tiles[group]
-            c_stats = work.tile([P, TILES_PER_GROUP, 6], F32)
-            for t in range(TILES_PER_GROUP):
-                nc.vector.bn_stats(out=c_stats[:, t, :], in_=kept["raw_c_rows"][:, t, :])
-            kept["c_stats"] = c_stats
+            moments = shared_tiles[group + CELL_LAG]["moments"]
+            nc.vector.bn_stats(
+                out=moments[:, GATE_STATS:ROUND_STATS, :].rearrange("p s m -> p (s m)"),
+                in_=kept_tiles[group]["raw_c"].rearrange("p t j -> p j t"),
+            )
 
         def cell_centre(group):
             if outside(group):
                 return
             kept = kept_tiles[group]
-            c_mean_var = work.tile([P, TILES_PER_GROUP, 2], F32)
-            for t in range(TILES_PER_GROUP):
-                nc.vector.bn_aggr(out=c_mean_var[:, t, :], in_=kept["c_stats"][:, t, :])
-            centred = work.tile([P, TILES_PER_GROUP, UNITS], F32, bufs=3)
-            for t in range(TILES_PER_GROUP):
+            centred = work.tile([P, TILES, UNITS], F32, bufs=4)
+            for t in range(TILES):
                 nc.vector.scalar_tensor_tensor(
                     out=centred[:, t, :],
-                    in0=kept["raw_c_rows"][:, t, :],
-                    scalar=c_mean_var[:, t, 0:1],
+                    in0=kept["raw_c"][:, t, :],
+                    scalar=shared_tiles[group + CELL_LAG]["moments"][:, GATE_STATS + t, 1:2],
                     in1=gamma_c_all,
                     op0=ALU.subtract,
                     op1=ALU.mult,
                 )
-            kept["c_mean_var"] = c_mean_var
             kept["centred"] = centred
-
-        def cell_variance(group):
-            if outside(group):
-                return
-            nc.vector.tensor_scalar_mul(
-                out=shared_tiles[group + CELL_LAG]["moments"][:, GROUP_STATS:ROUND_STATS],
-                in0=kept_tiles[group]["c_mean_var"][:, :, 1],
-                scalar1=float(UNITS**3),
-            )
 
         def cell_out(group):
             if outside(group):
                 return
             kept = kept_tiles[group]
-            new_c = work.tile([P, TILES_PER_GROUP, UNITS], F32, bufs=3)
-            for t in range(TILES_PER_GROUP):
+            new_c = work.tile([P, TILES, UNITS], F32, bufs=3)
+            for t in range(TILES):
                 nc.vector.scalar_tensor_tensor(
                     out=new_c[:, t, :],
                     in0=kept["centred"][:, t, :],
-                    scalar=shared_tiles[group + CELL_LAG]["inv"][:, GROUP_STATS + t : GROUP_STATS + t + 1],
+                    scalar=shared_tiles[group + CELL_LAG]["inv"][:, GATE_STATS + t : GATE_STATS + t + 1],
                     in1=beta_c_all,
                     op0=ALU.mult,
                     op1=ALU.add,
                 )
             kept["new_c"] = new_c[:].rearrange("p t j -> p (t j)")
-            nc.sync.dma_start(out=new_c_rows[:, group * GROUP_COLS : (group + 1) * GROUP_COLS], in_=kept["new_c"])
+            nc.sync.dma_start(out=new_c_rows[:, group * COLS : (group + 1) * COLS], in_=kept["new_c"])
 
         def cell_tanh(group):
             if outside(group):
                 return
             kept = kept_tiles[group]
-            tanh_c = work.tile([P, GROUP_COLS], F32)
+            tanh_c = work.tile([P, COLS], F32)
             nc.scalar.activation(out=tanh_c[:], in_=kept["new_c"], func=ACT.Tanh)
             kept["tanh_c"] = tanh_c
 
@@ -540,46 +504,43 @@ def tile_hyperlstmcell_pa_t_kernel(
             if outside(group):
                 return
             kept = kept_tiles[group]
-            new_h = work.tile([P, GROUP_COLS], F32, bufs=3)
+            new_h = work.tile([P, COLS], F32, bufs=3)
             nc.vector.tensor_tensor(
-                out=new_h[:],
-                in0=kept["gate_o_rows"].rearrange("p t j -> p (t j)"),
-                in1=kept["tanh_c"][:],
-                op=ALU.mult,
+                out=new_h[:], in0=kept["gate_o_rows"].rearrange("p t j -> p (t j)"), in1=kept["tanh_c"][:], op=ALU.mult
             )
-            nc.sync.dma_start(out=new_h_rows[:, group * GROUP_COLS : (group + 1) * GROUP_COLS], in_=new_h[:])
+            nc.sync.dma_start(out=new_h_rows[:, group * COLS : (group + 1) * COLS], in_=new_h[:])
 
         with tc.manual_schedule():
-            for i in range(-2, N_GROUPS + 6):
-                load(i + 4)
-                new_moments(i)
-                activate(i - 2)
-                add_bias(i, 0)
-                plain_product(i, 1)
-                cell_parts(i - 2)
-                cell_moments(i - 3)
-                hidden_out(i - 6)
-                cell_tanh(i - 5)
-                transpose_inputs(i + 2)
-                add_products(i, 0)
-                copy_inputs(i + 2)
-                mx_product(i + 1, 0)
-                add_bias(i, 1)
-                plain_product(i + 1, 0)
-                cell_centre(i - 3)
-                sum_squares(i, 0)
-                add_products(i, 1)
-                mx_product(i + 1, 1)
-                sum_squares(i, 1)
-                cell_variance(i - 3)
-                roots(i)
-                std_eps(i - 1)
+            for i in range(-4, N_GROUPS + 5):
+                load(i + 6)
+                new_moments(i + 1)
+                copy_u(i + 3)
                 quantise(i + 2)
                 inv_std(i - 1)
-                cell_sum(i - 2)
-                transpose_back(i - 2, i - 5)
                 gate_shift(i - 1)
-                normalise_on_scalar(i - 1)
                 cell_out(i - 4)
+                form_v(i, 0)
+                transpose_normed(i - 2, 1)
+                activate(i - 2, 1)
+                form_v(i, 1)
+                transpose_states(i + 1, i - 2)
+                copy_hyper_h(i + 1)
+                add_bias(i + 1, 0)
+                gate_moments(i, 0)
+                gate_moments(i, 1)
+                new_part(i - 2)
+                old_part(i - 2)
+                mx_product(i + 1, 1)
+                normalise_on_scalar(i - 1)
                 normalise_on_vector(i - 1)
-                transpose_normed(i - 1)
+                roots(i)
+                cell_tanh(i - 4)
+                add_bias(i + 1, 1)
+                transpose_u(i + 4)
+                transpose_back(i - 2, i - 4)
+                hidden_out(i - 4)
+                cell_moments(i - 2)
+                cell_centre(i - 2)
+                transpose_normed(i - 1, 0)
+                activate(i - 1, 0)
+                mx_product(i + 2, 0)

@@ -29,12 +29,15 @@ WORDS = K // 2
 GATE_FUNCS = (ACT.Sigmoid, ACT.Sigmoid, ACT.Tanh, ACT.Sigmoid)
 INPUT, FORGET, CELL, OUTPUT = range(GATES)
 
-CELL_LAG = 3
+CELL_LAG = 4
 ROUND_STATS = GATE_STATS + TILES
 
 LOADS_AHEAD = 6
 
 SCALAR_GATES = 3
+
+MX_ORDER = (0, 1, 0, 1)
+WARM_UP = 10
 
 FLOPS = 2 * BATCH * K * GATES * UNITS + 2 * BATCH * UNITS * GATES * UNITS
 
@@ -127,6 +130,11 @@ def tile_hyperlstmcell_pa_t_kernel(
         load(0)
         load(1)
 
+        half = const.tile([P, ROUND_STATS], F32)
+        nc.vector.memset(half[:], 0.5)
+        table = const.tile([P, 1], F32)
+        nc.scalar.activation(out=table[:], in_=half[:, 0:1], func=ACT.Sigmoid)
+
         ident_f32 = const.tile([P, P], F32)
         make_identity(nc, ident_f32[:])
         ident_bf16 = const.tile([P, P], BF16)
@@ -156,6 +164,18 @@ def tile_hyperlstmcell_pa_t_kernel(
             group_words(nc, wih_t_ps, wih_grouped[:, 2 * pair * P * 4 : (2 * pair + 2) * P * 4])
         nc.vector.quantize_mx(out=wih_codes[:].bitcast(FP8X4), scales=wih_scales[:], in_=wih_grouped[:])
 
+        warm = psum_v.tile([P, GATES * P], F32, tag="v")
+        for repeat in range(WARM_UP):
+            nc.tensor.matmul_mx(
+                out=warm[:],
+                lhsT=wih_codes[:, 0:P].bitcast(FP8X4),
+                lhsT_scale=wih_scales[:, 0:P],
+                rhs=wih_codes[:].bitcast(FP8X4),
+                rhs_scale=wih_scales[:],
+                start=True,
+                stop=True,
+            )
+
         cols_ps = psum_v.tile([P, P], BF16, tag="v")
         nc.tensor.transpose(cols_ps[:], rows[:], ident_bf16[:])
         cols = const.tile([P, 3 * GATES + 2], F32)
@@ -180,8 +200,6 @@ def tile_hyperlstmcell_pa_t_kernel(
         gamma_c_all = cell_all[:, 0, :]
         beta_c_all = cell_all[:, 1, :]
 
-        half = const.tile([P, ROUND_STATS], F32)
-        nc.vector.memset(half[:], 0.5)
 
         def transpose_u(group):
             if outside(group):
@@ -215,7 +233,7 @@ def tile_hyperlstmcell_pa_t_kernel(
                 return
             kept = kept_tiles[group]
             mx = psum_mx.tile([P, 2, COLS], F32)
-            for e in range(2):
+            for e in MX_ORDER:
                 g = 2 * pair + e
                 nc.tensor.matmul_mx(
                     out=mx[:, e, :],
@@ -233,7 +251,7 @@ def tile_hyperlstmcell_pa_t_kernel(
                 return
             kept = kept_tiles[group]
             if pair == 0:
-                mx_bias = work.tile([P, GATES, COLS], F32)
+                mx_bias = work.tile([P, GATES, COLS], F32, bufs=3)
                 kept["mx_bias"] = mx_bias
             for e in range(2):
                 g = 2 * pair + e
@@ -247,19 +265,26 @@ def tile_hyperlstmcell_pa_t_kernel(
         def transpose_states(early, late):
             if outside(early) and outside(late):
                 return
-            states = psum_in.tile([P, 2, COLS], BF16, tag="in")
+            states = psum_in.tile([P, COLS + COLS // 2], F32, tag="in")
+            hyper_h_ps = states[:, COLS:].bitcast(BF16)
             for t in range(TILES):
                 part = slice(t * P, (t + 1) * P)
                 if not outside(early):
-                    nc.tensor.transpose(states[:, 0, part], kept_tiles[early]["hyper_h_sb"][:, part], ident_bf16[:])
+                    nc.tensor.transpose(hyper_h_ps[:, part], kept_tiles[early]["hyper_h_sb"][:, part], ident_bf16[:])
             for t in range(TILES):
                 part = slice(t * P, (t + 1) * P)
                 if not outside(late):
-                    nc.tensor.transpose(states[:, 1, part], kept_tiles[late]["hyper_c_sb"][:, part], ident_bf16[:])
+                    nc.tensor.matmul(
+                        out=states[:, part],
+                        lhsT=kept_tiles[late]["hyper_c_sb"][:, part],
+                        rhs=ident_bf16[:],
+                        start=True,
+                        stop=True,
+                    )
             if not outside(early):
-                kept_tiles[early]["hyper_h_ps"] = states[:, 0, :]
+                kept_tiles[early]["hyper_h_ps"] = hyper_h_ps
             if not outside(late):
-                kept_tiles[late]["hyper_c_ps"] = states[:, 1, :]
+                kept_tiles[late]["hyper_c_ps"] = states[:, 0:COLS]
 
         def copy_hyper_h(group):
             if outside(group):
@@ -511,36 +536,36 @@ def tile_hyperlstmcell_pa_t_kernel(
             nc.sync.dma_start(out=new_h_rows[:, group * COLS : (group + 1) * COLS], in_=new_h[:])
 
         with tc.manual_schedule():
-            for i in range(-4, N_GROUPS + 5):
+            for i in range(-4, N_GROUPS + 7):
                 load(i + 6)
-                new_moments(i + 1)
-                copy_u(i + 3)
-                quantise(i + 2)
-                inv_std(i - 1)
-                gate_shift(i - 1)
-                cell_out(i - 4)
+                new_moments(i)
+                copy_hyper_h(i + 1)
+                mx_product(i + 2, 0)
+                activate(i - 2, 0)
+                cell_moments(i - 4)
+                hidden_out(i - 6)
+                cell_centre(i - 4)
+                old_part(i - 3)
                 form_v(i, 0)
+                add_bias(i + 2, 0)
+                new_part(i - 3)
                 transpose_normed(i - 2, 1)
                 activate(i - 2, 1)
                 form_v(i, 1)
-                transpose_states(i + 1, i - 2)
-                copy_hyper_h(i + 1)
-                add_bias(i + 1, 0)
                 gate_moments(i, 0)
+                inv_std(i - 1)
+                quantise(i + 3)
+                gate_shift(i - 1)
+                cell_out(i - 5)
                 gate_moments(i, 1)
-                new_part(i - 2)
-                old_part(i - 2)
-                mx_product(i + 1, 1)
+                transpose_u(i + 4)
                 normalise_on_scalar(i - 1)
+                copy_u(i + 4)
+                mx_product(i + 2, 1)
                 normalise_on_vector(i - 1)
                 roots(i)
-                cell_tanh(i - 4)
-                add_bias(i + 1, 1)
-                transpose_u(i + 4)
-                transpose_back(i - 2, i - 4)
-                hidden_out(i - 4)
-                cell_moments(i - 2)
-                cell_centre(i - 2)
+                transpose_back(i - 3, i - 5)
+                add_bias(i + 2, 1)
+                cell_tanh(i - 5)
+                transpose_states(i + 2, i - 2)
                 transpose_normed(i - 1, 0)
-                activate(i - 1, 0)
-                mx_product(i + 2, 0)

@@ -36,22 +36,21 @@ LOADS_AHEAD = 6
 
 SCALAR_GATES = 3
 
-MX_ORDER = (0, 1, 0, 1)
-WARM_UP = 10
+MX_ORDER = ((0, 1), (0, 1, 0, 1))
 
 FLOPS = 2 * BATCH * K * GATES * UNITS + 2 * BATCH * UNITS * GATES * UNITS
 
 
-def transpose_words(nc, psum, ident_f32, words):
-    k_first = psum.tile([P, 2, 2, P], F32, tag="in")
+def transpose_words(nc, psum, tag, ident_f32, words):
+    k_first = psum.tile([P, 2, 2, P], F32, tag=tag)
     for i in range(2):
         for u in range(2):
             nc.tensor.transpose(k_first[:, i, u, :], words[i][:, u::2], ident_f32)
     return k_first
 
 
-def group_words(nc, k_first, grouped):
-    nc.scalar.copy(
+def group_words(copy, k_first, grouped):
+    copy(
         out=grouped.bitcast(F32).rearrange("p (i r u) -> p i r u", i=2, u=2),
         in_=k_first[:].rearrange("p i u r -> p i r u"),
     )
@@ -104,6 +103,14 @@ def tile_hyperlstmcell_pa_t_kernel(
             last = ROUND_STATS if r >= CELL_LAG else GATE_STATS
             return slice(first, last)
 
+        wih_rows = const.tile([P, GATES * K], BF16)
+
+        def load_weights():
+            nc.sync.dma_start(
+                out=wih_rows[:].rearrange("p (g k) -> p g k", g=GATES),
+                in_=hc_Wih.rearrange("(g p) k -> p g k", p=P),
+            )
+
         def load(group):
             if outside(group):
                 return
@@ -114,92 +121,86 @@ def tile_hyperlstmcell_pa_t_kernel(
             u_parts = u_sb[:].rearrange("p (t s k) -> p t s k", t=TILES, s=2)
             wide = slice(group * TILES * IN, (group + 1) * TILES * IN)
             narrow = slice(group * COLS, (group + 1) * COLS)
-            nc.sync.dma_start(out=u_parts[:, :, 0, :], in_=x_rows[:, wide].rearrange("p (t k) -> p t k", t=TILES))
-            nc.sync.dma_start(out=u_parts[:, :, 1, :], in_=h_rows[:, wide].rearrange("p (t k) -> p t k", t=TILES))
-            nc.sync.dma_start(out=hyper_h_sb[:], in_=hyper_h_rows[:, narrow])
-            nc.sync.dma_start(out=hyper_c_sb[:], in_=hyper_c_rows[:, narrow])
             kept["u_sb"] = u_sb
             kept["hyper_h_sb"] = hyper_h_sb
             kept["hyper_c_sb"] = hyper_c_sb
-
-        wih_rows = const.tile([P, GATES * K], BF16)
-        nc.sync.dma_start(
-            out=wih_rows[:].rearrange("p (g k) -> p g k", g=GATES),
-            in_=hc_Wih.rearrange("(g p) k -> p g k", p=P),
-        )
-        load(0)
-        load(1)
+            nc.sync.dma_start(out=u_parts[:, :, 0, :], in_=x_rows[:, wide].rearrange("p (t k) -> p t k", t=TILES))
+            nc.sync.dma_start(out=u_parts[:, :, 1, :], in_=h_rows[:, wide].rearrange("p (t k) -> p t k", t=TILES))
+            if group == 0:
+                load_weights()
+            nc.sync.dma_start(out=hyper_h_sb[:], in_=hyper_h_rows[:, narrow])
+            nc.sync.dma_start(out=hyper_c_sb[:], in_=hyper_c_rows[:, narrow])
 
         half = const.tile([P, ROUND_STATS], F32)
         nc.vector.memset(half[:], 0.5)
         table = const.tile([P, 1], F32)
         nc.scalar.activation(out=table[:], in_=half[:, 0:1], func=ACT.Sigmoid)
+        load(0)
+
+        rows = const.tile([P, P], BF16)
+        nc.vector.memset(rows[:], 0.0)
+        nc.scalar.dma_start(out=rows[2 * GATES : 3 * GATES, :], in_=hc_bih.rearrange("(g j) -> g j", g=GATES))
+        nc.scalar.dma_start(out=rows[0:GATES, :], in_=hc_ln_gamma)
+        nc.scalar.dma_start(out=rows[GATES : 2 * GATES, :], in_=hc_ln_beta)
+        nc.scalar.dma_start(out=rows[3 * GATES : 3 * GATES + 1, :], in_=hc_lnc_gamma.rearrange("(o n) -> o n", o=1))
+        nc.scalar.dma_start(out=rows[3 * GATES + 1 : 3 * GATES + 2, :], in_=hc_lnc_beta.rearrange("(o n) -> o n", o=1))
+        whh_rows = const.tile([P, GATES * UNITS], BF16)
+        nc.sync.dma_start(
+            out=whh_rows[:].rearrange("p (g k) -> p g k", g=GATES),
+            in_=hc_Whh.rearrange("(g p) k -> p g k", p=P),
+        )
+        load(1)
+        load(2)
 
         ident_f32 = const.tile([P, P], F32)
         make_identity(nc, ident_f32[:])
         ident_bf16 = const.tile([P, P], BF16)
         nc.vector.tensor_copy(out=ident_bf16[:], in_=ident_f32[:])
-
-        rows = const.tile([P, P], BF16)
-        nc.vector.memset(rows[:], 0.0)
-        nc.scalar.dma_start(out=rows[0:GATES, :], in_=hc_ln_gamma)
-        nc.scalar.dma_start(out=rows[GATES : 2 * GATES, :], in_=hc_ln_beta)
-        nc.scalar.dma_start(out=rows[2 * GATES : 3 * GATES, :], in_=hc_bih.rearrange("(g j) -> g j", g=GATES))
-        nc.scalar.dma_start(out=rows[3 * GATES : 3 * GATES + 1, :], in_=hc_lnc_gamma.rearrange("(o n) -> o n", o=1))
-        nc.scalar.dma_start(out=rows[3 * GATES + 1 : 3 * GATES + 2, :], in_=hc_lnc_beta.rearrange("(o n) -> o n", o=1))
-        whh_rows = const.tile([P, GATES * UNITS], BF16)
-        nc.scalar.dma_start(
-            out=whh_rows[:].rearrange("p (g k) -> p g k", g=GATES),
-            in_=hc_Whh.rearrange("(g p) k -> p g k", p=P),
-        )
-
-        wih_words = wih_rows[:].bitcast(F32)
-        wih_grouped = const.tile([P, GATES * P * 4], BF16, align_bytes=64)
         wih_codes = const.tile([P, GATES * P], U32, align_bytes=64)
         wih_scales = const.tile([P, GATES * P], U8, align_bytes=64)
-        for pair in range(GATES // 2):
-            wih_t_ps = transpose_words(
-                nc, psum_in, ident_f32[:], [wih_words[:, g * WORDS : (g + 1) * WORDS] for g in (2 * pair, 2 * pair + 1)]
-            )
-            group_words(nc, wih_t_ps, wih_grouped[:, 2 * pair * P * 4 : (2 * pair + 2) * P * 4])
-        nc.vector.quantize_mx(out=wih_codes[:].bitcast(FP8X4), scales=wih_scales[:], in_=wih_grouped[:])
-
-        warm = psum_v.tile([P, GATES * P], F32, tag="v")
-        for repeat in range(WARM_UP):
-            nc.tensor.matmul_mx(
-                out=warm[:],
-                lhsT=wih_codes[:, 0:P].bitcast(FP8X4),
-                lhsT_scale=wih_scales[:, 0:P],
-                rhs=wih_codes[:].bitcast(FP8X4),
-                rhs_scale=wih_scales[:],
-                start=True,
-                stop=True,
-            )
-
-        cols_ps = psum_v.tile([P, P], BF16, tag="v")
-        nc.tensor.transpose(cols_ps[:], rows[:], ident_bf16[:])
         cols = const.tile([P, 3 * GATES + 2], F32)
-        nc.vector.tensor_copy(out=cols[:], in_=cols_ps[:, 0 : 3 * GATES + 2])
-        forget_beta = cols[:, GATES + FORGET : GATES + FORGET + 1]
-        nc.vector.tensor_scalar_add(out=forget_beta, in0=forget_beta, scalar1=1.0)
-
-        whh_t_ps = psum_v.tile([P, GATES * P], BF16, tag="v")
-        for g in range(GATES):
-            nc.tensor.transpose(
-                whh_t_ps[:, g * P : (g + 1) * P], whh_rows[:, g * UNITS : (g + 1) * UNITS], ident_bf16[:]
-            )
         whh_t = const.tile([P, GATES * P], BF16)
-        nc.vector.tensor_copy(out=whh_t[:], in_=whh_t_ps[:])
-
-        cell_ps = psum_v.tile([P, 2, UNITS], F32, tag="v")
-        for c in range(2):
-            col = cols[:, 3 * GATES + c : 3 * GATES + c + 1]
-            nc.tensor.transpose(cell_ps[:, c, :], col.to_broadcast([P, P]), ident_f32[:])
         cell_all = const.tile([P, 2, UNITS], F32)
-        nc.vector.tensor_copy(out=cell_all[:], in_=cell_ps[:])
         gamma_c_all = cell_all[:, 0, :]
         beta_c_all = cell_all[:, 1, :]
 
+        def transpose_wih(pair):
+            wih_words = wih_rows[:].bitcast(F32)
+            return transpose_words(
+                nc,
+                psum_v,
+                "v",
+                ident_f32[:],
+                [wih_words[:, g * WORDS : (g + 1) * WORDS] for g in (2 * pair, 2 * pair + 1)],
+            )
+
+        def quantise_wih(copy, pair, wih_t):
+            wih_grouped = const.tile([P, 2 * P * 4], BF16, align_bytes=64, tag="wih_grouped", bufs=2)
+            group_words(copy, wih_t, wih_grouped[:])
+            part = slice(2 * pair * P, (2 * pair + 2) * P)
+            nc.vector.quantize_mx(out=wih_codes[:, part].bitcast(FP8X4), scales=wih_scales[:, part], in_=wih_grouped[:])
+
+        def vector_columns():
+            cols_ps = psum_v.tile([P, P], BF16, tag="v")
+            nc.tensor.transpose(cols_ps[:], rows[:], ident_bf16[:])
+            nc.vector.tensor_copy(out=cols[:], in_=cols_ps[:, 0 : 3 * GATES + 2])
+            forget_beta = cols[:, GATES + FORGET : GATES + FORGET + 1]
+            nc.vector.tensor_scalar_add(out=forget_beta, in0=forget_beta, scalar1=1.0)
+
+        def transpose_whh():
+            whh_t_ps = psum_v.tile([P, GATES * P], BF16, tag="v")
+            for g in range(GATES):
+                nc.tensor.transpose(
+                    whh_t_ps[:, g * P : (g + 1) * P], whh_rows[:, g * UNITS : (g + 1) * UNITS], ident_bf16[:]
+                )
+            nc.vector.tensor_copy(out=whh_t[:], in_=whh_t_ps[:])
+
+        def spread_cell_vectors():
+            cell_ps = psum_v.tile([P, 2, UNITS], F32, tag="v")
+            for c in range(2):
+                col = cols[:, 3 * GATES + c : 3 * GATES + c + 1]
+                nc.tensor.transpose(cell_ps[:, c, :], col.to_broadcast([P, P]), ident_f32[:])
+            nc.vector.tensor_copy(out=cell_all[:], in_=cell_ps[:])
 
         def transpose_u(group):
             if outside(group):
@@ -207,7 +208,7 @@ def tile_hyperlstmcell_pa_t_kernel(
             kept = kept_tiles[group]
             u_words = kept["u_sb"][:].bitcast(F32)
             kept["u_t"] = transpose_words(
-                nc, psum_in, ident_f32[:], [u_words[:, t * WORDS : (t + 1) * WORDS] for t in range(TILES)]
+                nc, psum_in, "in", ident_f32[:], [u_words[:, t * WORDS : (t + 1) * WORDS] for t in range(TILES)]
             )
 
         def copy_u(group):
@@ -215,7 +216,7 @@ def tile_hyperlstmcell_pa_t_kernel(
                 return
             kept = kept_tiles[group]
             u_grouped = work.tile([P, COLS * 4], BF16, align_bytes=64)
-            group_words(nc, kept["u_t"], u_grouped[:])
+            group_words(nc.scalar.copy, kept["u_t"], u_grouped[:])
             kept["u_grouped"] = u_grouped
 
         def quantise(group):
@@ -233,7 +234,7 @@ def tile_hyperlstmcell_pa_t_kernel(
                 return
             kept = kept_tiles[group]
             mx = psum_mx.tile([P, 2, COLS], F32)
-            for e in MX_ORDER:
+            for e in MX_ORDER[pair]:
                 g = 2 * pair + e
                 nc.tensor.matmul_mx(
                     out=mx[:, e, :],
@@ -262,15 +263,12 @@ def tile_hyperlstmcell_pa_t_kernel(
                     bias=cols[:, 2 * GATES + g : 2 * GATES + g + 1],
                 )
 
-        def transpose_states(early, late):
+        def states_and_mx(early, late, mx_group):
             if outside(early) and outside(late):
+                mx_product(mx_group, 1)
                 return
             states = psum_in.tile([P, COLS + COLS // 2], F32, tag="in")
             hyper_h_ps = states[:, COLS:].bitcast(BF16)
-            for t in range(TILES):
-                part = slice(t * P, (t + 1) * P)
-                if not outside(early):
-                    nc.tensor.transpose(hyper_h_ps[:, part], kept_tiles[early]["hyper_h_sb"][:, part], ident_bf16[:])
             for t in range(TILES):
                 part = slice(t * P, (t + 1) * P)
                 if not outside(late):
@@ -281,6 +279,12 @@ def tile_hyperlstmcell_pa_t_kernel(
                         start=True,
                         stop=True,
                     )
+                if t == 0:
+                    mx_product(mx_group, 1)
+            for t in range(TILES):
+                part = slice(t * P, (t + 1) * P)
+                if not outside(early):
+                    nc.tensor.transpose(hyper_h_ps[:, part], kept_tiles[early]["hyper_h_sb"][:, part], ident_bf16[:])
             if not outside(early):
                 kept_tiles[early]["hyper_h_ps"] = hyper_h_ps
             if not outside(late):
@@ -294,7 +298,7 @@ def tile_hyperlstmcell_pa_t_kernel(
             nc.scalar.copy(out=hyper_h_t[:], in_=kept["hyper_h_ps"])
             kept["hyper_h_t"] = hyper_h_t
 
-        def form_v(group, t):
+        def plain_product(group, t):
             if outside(group):
                 return
             kept = kept_tiles[group]
@@ -306,16 +310,21 @@ def tile_hyperlstmcell_pa_t_kernel(
                 start=True,
                 stop=False,
             )
+            kept["v", t] = v
+
+        def add_mx_product(group, t):
+            if outside(group):
+                return
+            kept = kept_tiles[group]
             for g in range(GATES):
                 nc.tensor.matmul(
-                    out=v[:, g, :],
+                    out=kept["v", t][:, g, :],
                     lhsT=kept["mx_bias"][:, g, t * P : (t + 1) * P],
                     rhs=ident_f32[:],
                     start=False,
                     stop=g == GATES - 1,
                     is_transpose=True,
                 )
-            kept["v", t] = v
 
         def new_moments(r):
             if no_round(r):
@@ -535,37 +544,55 @@ def tile_hyperlstmcell_pa_t_kernel(
             )
             nc.sync.dma_start(out=new_h_rows[:, group * COLS : (group + 1) * COLS], in_=new_h[:])
 
+        def head():
+            transpose_u(0)
+            copy_u(0)
+            wih_first = transpose_wih(0)
+            quantise(0)
+            quantise_wih(nc.vector.tensor_copy, 0, wih_first)
+            wih_second = transpose_wih(1)
+            states_and_mx(0, -1, -1)
+            quantise_wih(nc.scalar.copy, 1, wih_second)
+            copy_hyper_h(0)
+            vector_columns()
+            transpose_whh()
+
+
         with tc.manual_schedule():
-            for i in range(-4, N_GROUPS + 7):
-                load(i + 6)
-                new_moments(i)
-                copy_hyper_h(i + 1)
-                mx_product(i + 2, 0)
-                activate(i - 2, 0)
-                cell_moments(i - 4)
-                hidden_out(i - 6)
-                cell_centre(i - 4)
+            head()
+            for i in range(-1, N_GROUPS + 8):
+                if i == 0:
+                    spread_cell_vectors()
+                load(i + 4)
+                new_moments(i + 1)
+                plain_product(i, 0)
+                plain_product(i, 1)
+                add_bias(i, 1)
+                mx_product(i + 1, 0)
                 old_part(i - 3)
-                form_v(i, 0)
-                add_bias(i + 2, 0)
-                new_part(i - 3)
-                transpose_normed(i - 2, 1)
-                activate(i - 2, 1)
-                form_v(i, 1)
-                gate_moments(i, 0)
+                activate(i - 2, 0)
+                add_mx_product(i, 0)
+                add_mx_product(i, 1)
+                add_bias(i + 1, 0)
                 inv_std(i - 1)
-                quantise(i + 3)
                 gate_shift(i - 1)
-                cell_out(i - 5)
+                new_part(i - 3)
+                gate_moments(i, 0)
                 gate_moments(i, 1)
-                transpose_u(i + 4)
                 normalise_on_scalar(i - 1)
-                copy_u(i + 4)
-                mx_product(i + 2, 1)
+                transpose_u(i + 2)
+                transpose_normed(i - 2, 1)
+                copy_u(i + 2)
                 normalise_on_vector(i - 1)
                 roots(i)
-                transpose_back(i - 3, i - 5)
-                add_bias(i + 2, 1)
-                cell_tanh(i - 5)
-                transpose_states(i + 2, i - 2)
+                activate(i - 2, 1)
+                transpose_back(i - 3, i - 6)
+                cell_moments(i - 3)
+                cell_tanh(i - 6)
+                cell_centre(i - 3)
+                cell_out(i - 5)
+                hidden_out(i - 6)
+                quantise(i + 2)
+                states_and_mx(i + 2, i - 2, i + 1)
+                copy_hyper_h(i + 2)
                 transpose_normed(i - 1, 0)

@@ -36,7 +36,7 @@ LOADS_AHEAD = 6
 
 SCALAR_GATES = 3
 
-MX_ORDER = ((0, 1), (0, 1, 0, 1))
+MX_ORDER = ((0, 1, 0, 1), (0, 1, 0, 1))
 
 FLOPS = 2 * BATCH * K * GATES * UNITS + 2 * BATCH * UNITS * GATES * UNITS
 
@@ -263,32 +263,36 @@ def tile_hyperlstmcell_pa_t_kernel(
                     bias=cols[:, 2 * GATES + g : 2 * GATES + g + 1],
                 )
 
-        def states_and_mx(early, late, mx_group):
-            if outside(early) and outside(late):
-                mx_product(mx_group, 1)
+        def transpose_hyper_h(group):
+            if outside(group):
                 return
-            states = psum_in.tile([P, COLS + COLS // 2], F32, tag="in")
+            states = new_states(group)
             hyper_h_ps = states[:, COLS:].bitcast(BF16)
             for t in range(TILES):
                 part = slice(t * P, (t + 1) * P)
-                if not outside(late):
-                    nc.tensor.matmul(
-                        out=states[:, part],
-                        lhsT=kept_tiles[late]["hyper_c_sb"][:, part],
-                        rhs=ident_bf16[:],
-                        start=True,
-                        stop=True,
-                    )
-                if t == 0:
-                    mx_product(mx_group, 1)
+                nc.tensor.transpose(hyper_h_ps[:, part], kept_tiles[group]["hyper_h_sb"][:, part], ident_bf16[:])
+            kept_tiles[group]["hyper_h_ps"] = hyper_h_ps
+
+        def new_states(group):
+            states = psum_in.tile([P, COLS + COLS // 2], F32, tag="in")
+            if not outside(group):
+                kept_tiles[group]["states"] = states
+            return states
+
+        def transpose_hyper_c(group, early):
+            if outside(group):
+                return
+            states = new_states(early) if outside(early) else kept_tiles[early]["states"]
             for t in range(TILES):
                 part = slice(t * P, (t + 1) * P)
-                if not outside(early):
-                    nc.tensor.transpose(hyper_h_ps[:, part], kept_tiles[early]["hyper_h_sb"][:, part], ident_bf16[:])
-            if not outside(early):
-                kept_tiles[early]["hyper_h_ps"] = hyper_h_ps
-            if not outside(late):
-                kept_tiles[late]["hyper_c_ps"] = states[:, 0:COLS]
+                nc.tensor.matmul(
+                    out=states[:, part],
+                    lhsT=kept_tiles[group]["hyper_c_sb"][:, part],
+                    rhs=ident_bf16[:],
+                    start=True,
+                    stop=True,
+                )
+            kept_tiles[group]["hyper_c_ps"] = states[:, 0:COLS]
 
         def copy_hyper_h(group):
             if outside(group):
@@ -343,16 +347,26 @@ def tile_hyperlstmcell_pa_t_kernel(
                     in_=kept_tiles[group]["v", t][:, 2 * pair : 2 * pair + 2, :].rearrange("p g j -> p j g"),
                 )
 
-        def roots(r):
+        def roots(r, part):
             if no_round(r):
                 return
             shared = shared_tiles[r]
             live_cols = live(r)
-            root = work.tile([P, ROUND_STATS], F32)
+            first = max(live_cols.start, GATES) if part else live_cols.start
+            last = live_cols.stop if part else min(live_cols.stop, GATES)
+            if first >= last:
+                return
+            live_cols = slice(first, last)
+            if part == 0 or r >= N_GROUPS:
+                root = work.tile([P, ROUND_STATS], F32)
+                std = work.tile([P, ROUND_STATS], F32)
+                shared["root"] = root
+                shared["std"] = std
+            root = shared["root"]
+            std = shared["std"]
             nc.gpsimd.tensor_tensor(
                 out=root[:, live_cols], in0=shared["moments"][:, live_cols, 2], in1=half[:, live_cols], op=ALU.pow
             )
-            std = work.tile([P, ROUND_STATS], F32)
             nc.gpsimd.tensor_scalar(
                 out=std[:, live_cols],
                 in0=root[:, live_cols],
@@ -361,7 +375,6 @@ def tile_hyperlstmcell_pa_t_kernel(
                 op0=ALU.mult,
                 op1=ALU.add,
             )
-            shared["std"] = std
 
         def inv_std(r):
             if no_round(r):
@@ -458,6 +471,14 @@ def tile_hyperlstmcell_pa_t_kernel(
             nc.gpsimd.tensor_tensor(out=new[:], in0=kept["gate", INPUT][:], in1=kept["gate", CELL][:], op=ALU.mult)
             kept["new"] = new
 
+        def cell_sum(group):
+            if outside(group):
+                return
+            kept = kept_tiles[group]
+            raw = work.tile([P, COLS], F32)
+            nc.gpsimd.tensor_tensor(out=raw[:], in0=kept["old"][:], in1=kept["new"][:], op=ALU.add)
+            kept["raw"] = raw
+
         def transpose_back(cell_group, gate_group):
             if outside(cell_group) and outside(gate_group):
                 return
@@ -469,16 +490,7 @@ def tile_hyperlstmcell_pa_t_kernel(
             for t in range(TILES):
                 part = slice(t * P, (t + 1) * P)
                 if not outside(cell_group):
-                    kept = kept_tiles[cell_group]
-                    for source, first in ((kept["old"], True), (kept["new"], False)):
-                        nc.tensor.matmul(
-                            out=back[:, 0, t, :],
-                            lhsT=source[:, part],
-                            rhs=ident_f32[:],
-                            start=first,
-                            stop=not first,
-                            is_transpose=True,
-                        )
+                    nc.tensor.transpose(back[:, 0, t, :], kept_tiles[cell_group]["raw"][:, part], ident_f32[:])
             if not outside(cell_group):
                 kept_tiles[cell_group]["raw_c"] = back[:, 0, :, :]
             if not outside(gate_group):
@@ -551,48 +563,50 @@ def tile_hyperlstmcell_pa_t_kernel(
             quantise(0)
             quantise_wih(nc.vector.tensor_copy, 0, wih_first)
             wih_second = transpose_wih(1)
-            states_and_mx(0, -1, -1)
             quantise_wih(nc.scalar.copy, 1, wih_second)
-            copy_hyper_h(0)
             vector_columns()
             transpose_whh()
 
 
         with tc.manual_schedule():
             head()
-            for i in range(-1, N_GROUPS + 8):
+            for i in range(-1, N_GROUPS + 7):
                 if i == 0:
                     spread_cell_vectors()
                 load(i + 4)
-                new_moments(i + 1)
+                new_moments(i)
+                transpose_u(i + 2)
+                copy_u(i + 2)
+                transpose_normed(i - 2, 0)
+                cell_moments(i - 4)
+                cell_centre(i - 4)
+                hidden_out(i - 6)
                 plain_product(i, 0)
                 plain_product(i, 1)
-                add_bias(i, 1)
                 mx_product(i + 1, 0)
-                old_part(i - 3)
                 activate(i - 2, 0)
+                inv_std(i - 1)
+                quantise(i + 2)
+                gate_shift(i - 1)
+                cell_out(i - 5)
                 add_mx_product(i, 0)
                 add_mx_product(i, 1)
                 add_bias(i + 1, 0)
-                inv_std(i - 1)
-                gate_shift(i - 1)
                 new_part(i - 3)
+                cell_sum(i - 3)
                 gate_moments(i, 0)
+                roots(i, 0)
                 gate_moments(i, 1)
                 normalise_on_scalar(i - 1)
-                transpose_u(i + 2)
                 transpose_normed(i - 2, 1)
-                copy_u(i + 2)
-                normalise_on_vector(i - 1)
-                roots(i)
                 activate(i - 2, 1)
-                transpose_back(i - 3, i - 6)
-                cell_moments(i - 3)
-                cell_tanh(i - 6)
-                cell_centre(i - 3)
-                cell_out(i - 5)
-                hidden_out(i - 6)
-                quantise(i + 2)
-                states_and_mx(i + 2, i - 2, i + 1)
-                copy_hyper_h(i + 2)
-                transpose_normed(i - 1, 0)
+                transpose_hyper_h(i + 1)
+                transpose_hyper_c(i - 2, i + 1)
+                old_part(i - 2)
+                normalise_on_vector(i - 1)
+                roots(i, 1)
+                mx_product(i + 1, 1)
+                copy_hyper_h(i + 1)
+                add_bias(i + 1, 1)
+                cell_tanh(i - 5)
+                transpose_back(i - 3, i - 5)

@@ -36,7 +36,9 @@ LOADS_AHEAD = 6
 
 SCALAR_GATES = 3
 
-MX_ORDER = ((0, 1, 0, 1), (0, 1, 0, 1))
+MX_ORDER = ((0, 1), (0, 1, 0, 1))
+COLD_GROUPS = 2
+LATE_GROUPS = 3
 
 FLOPS = 2 * BATCH * K * GATES * UNITS + 2 * BATCH * UNITS * GATES * UNITS
 
@@ -234,7 +236,7 @@ def tile_hyperlstmcell_pa_t_kernel(
                 return
             kept = kept_tiles[group]
             mx = psum_mx.tile([P, 2, COLS], F32)
-            for e in MX_ORDER[pair]:
+            for e in (0, 1) if group < COLD_GROUPS else MX_ORDER[pair]:
                 g = 2 * pair + e
                 nc.tensor.matmul_mx(
                     out=mx[:, e, :],
@@ -347,34 +349,32 @@ def tile_hyperlstmcell_pa_t_kernel(
                     in_=kept_tiles[group]["v", t][:, 2 * pair : 2 * pair + 2, :].rearrange("p g j -> p j g"),
                 )
 
-        def roots(r, part):
+        def roots(r):
             if no_round(r):
                 return
             shared = shared_tiles[r]
             live_cols = live(r)
-            first = max(live_cols.start, GATES) if part else live_cols.start
-            last = live_cols.stop if part else min(live_cols.stop, GATES)
-            if first >= last:
-                return
-            live_cols = slice(first, last)
-            if part == 0 or r >= N_GROUPS:
-                root = work.tile([P, ROUND_STATS], F32)
-                std = work.tile([P, ROUND_STATS], F32)
-                shared["root"] = root
-                shared["std"] = std
-            root = shared["root"]
-            std = shared["std"]
+            root = work.tile([P, ROUND_STATS], F32)
             nc.gpsimd.tensor_tensor(
                 out=root[:, live_cols], in0=shared["moments"][:, live_cols, 2], in1=half[:, live_cols], op=ALU.pow
             )
-            nc.gpsimd.tensor_scalar(
+            shared["root"] = root
+
+        def std_eps(r):
+            if no_round(r):
+                return
+            shared = shared_tiles[r]
+            live_cols = live(r)
+            std = work.tile([P, ROUND_STATS], F32)
+            nc.vector.tensor_scalar(
                 out=std[:, live_cols],
-                in0=root[:, live_cols],
+                in0=shared["root"][:, live_cols],
                 scalar1=1.0 / (UNITS - 1) ** 0.5,
                 scalar2=EPS,
                 op0=ALU.mult,
                 op1=ALU.add,
             )
+            shared["std"] = std
 
         def inv_std(r):
             if no_round(r):
@@ -433,7 +433,10 @@ def tile_hyperlstmcell_pa_t_kernel(
             if outside(group):
                 return
             kept = kept_tiles[group]
-            norm = psum_norm.tile([P, 2, TILES, P], F32)
+            if pair and group >= N_GROUPS - 2:
+                norm = psum_v.tile([P, 2, TILES, P], F32, tag="v")
+            else:
+                norm = psum_norm.tile([P, 2, TILES, P], F32)
             for e in range(2):
                 for t in range(TILES):
                     nc.tensor.transpose(norm[:, e, t, :], kept["normed"][:, t, 2 * pair + e, :], ident_f32[:])
@@ -471,30 +474,37 @@ def tile_hyperlstmcell_pa_t_kernel(
             nc.gpsimd.tensor_tensor(out=new[:], in0=kept["gate", INPUT][:], in1=kept["gate", CELL][:], op=ALU.mult)
             kept["new"] = new
 
-        def cell_sum(group):
-            if outside(group):
-                return
-            kept = kept_tiles[group]
-            raw = work.tile([P, COLS], F32)
-            nc.gpsimd.tensor_tensor(out=raw[:], in0=kept["old"][:], in1=kept["new"][:], op=ALU.add)
-            kept["raw"] = raw
+        def transpose_rows(out, tiles):
+            for t in range(TILES):
+                for n, tile in enumerate(tiles):
+                    nc.tensor.matmul(
+                        out=out[:, t, :],
+                        lhsT=tile[:, t * P : (t + 1) * P],
+                        rhs=ident_f32[:],
+                        start=n == 0,
+                        stop=n == len(tiles) - 1,
+                        is_transpose=True,
+                    )
 
         def transpose_back(cell_group, gate_group):
-            if outside(cell_group) and outside(gate_group):
+            if not outside(cell_group) and cell_group >= N_GROUPS - LATE_GROUPS:
+                late = psum_v.tile([P, 2, TILES, UNITS], F32, tag="v")
+                kept = kept_tiles[cell_group]
+                transpose_rows(late[:, 1, :, :], [kept["gate", OUTPUT]])
+                transpose_rows(late[:, 0, :, :], [kept["old"], kept["new"]])
+                kept["raw_c"] = late[:, 0, :, :]
+                kept["gate_o_rows"] = late[:, 1, :, :]
+            has_cell = 0 <= cell_group < N_GROUPS - LATE_GROUPS
+            has_gate = 0 <= gate_group < N_GROUPS - LATE_GROUPS
+            if not has_cell and not has_gate:
                 return
             back = psum_back.tile([P, 2, TILES, UNITS], F32)
-            for t in range(TILES):
-                part = slice(t * P, (t + 1) * P)
-                if not outside(gate_group):
-                    nc.tensor.transpose(back[:, 1, t, :], kept_tiles[gate_group]["gate", OUTPUT][:, part], ident_f32[:])
-            for t in range(TILES):
-                part = slice(t * P, (t + 1) * P)
-                if not outside(cell_group):
-                    nc.tensor.transpose(back[:, 0, t, :], kept_tiles[cell_group]["raw"][:, part], ident_f32[:])
-            if not outside(cell_group):
-                kept_tiles[cell_group]["raw_c"] = back[:, 0, :, :]
-            if not outside(gate_group):
+            if has_gate:
+                transpose_rows(back[:, 1, :, :], [kept_tiles[gate_group]["gate", OUTPUT]])
                 kept_tiles[gate_group]["gate_o_rows"] = back[:, 1, :, :]
+            if has_cell:
+                transpose_rows(back[:, 0, :, :], [kept_tiles[cell_group]["old"], kept_tiles[cell_group]["new"]])
+                kept_tiles[cell_group]["raw_c"] = back[:, 0, :, :]
 
         def cell_moments(group):
             if outside(group):
@@ -570,7 +580,7 @@ def tile_hyperlstmcell_pa_t_kernel(
 
         with tc.manual_schedule():
             head()
-            for i in range(-1, N_GROUPS + 7):
+            for i in range(-1, N_GROUPS + 3):
                 if i == 0:
                     spread_cell_vectors()
                 load(i + 4)
@@ -585,28 +595,43 @@ def tile_hyperlstmcell_pa_t_kernel(
                 plain_product(i, 1)
                 mx_product(i + 1, 0)
                 activate(i - 2, 0)
-                inv_std(i - 1)
-                quantise(i + 2)
-                gate_shift(i - 1)
-                cell_out(i - 5)
                 add_mx_product(i, 0)
                 add_mx_product(i, 1)
-                add_bias(i + 1, 0)
-                new_part(i - 3)
-                cell_sum(i - 3)
-                gate_moments(i, 0)
-                roots(i, 0)
-                gate_moments(i, 1)
-                normalise_on_scalar(i - 1)
-                transpose_normed(i - 2, 1)
-                activate(i - 2, 1)
                 transpose_hyper_h(i + 1)
                 transpose_hyper_c(i - 2, i + 1)
-                old_part(i - 2)
-                normalise_on_vector(i - 1)
-                roots(i, 1)
-                mx_product(i + 1, 1)
+                add_bias(i + 1, 0)
                 copy_hyper_h(i + 1)
+                new_part(i - 3)
+                gate_moments(i, 0)
+                quantise(i + 2)
+                std_eps(i - 1)
+                gate_moments(i, 1)
+                inv_std(i - 1)
+                transpose_normed(i - 2, 1)
+                activate(i - 2, 1)
+                old_part(i - 2)
+                gate_shift(i - 1)
+                normalise_on_scalar(i - 1)
+                normalise_on_vector(i - 1)
+                roots(i)
+                mx_product(i + 1, 1)
                 add_bias(i + 1, 1)
+                cell_out(i - 5)
                 cell_tanh(i - 5)
                 transpose_back(i - 3, i - 5)
+            last = N_GROUPS - 1
+            new_moments(last + CELL_LAG)
+            std_eps(last - 1 + CELL_LAG)
+            cell_moments(last)
+            inv_std(last - 1 + CELL_LAG)
+            roots(last + CELL_LAG)
+            cell_centre(last)
+            cell_out(last - 1)
+            hidden_out(last - 2)
+            cell_tanh(last - 1)
+            std_eps(last + CELL_LAG)
+            inv_std(last + CELL_LAG)
+            hidden_out(last - 1)
+            cell_out(last)
+            cell_tanh(last)
+            hidden_out(last)

@@ -37,7 +37,7 @@ LOADS_AHEAD = 6
 SCALAR_GATES = 3
 
 MX_ORDER = ((0, 1), (0, 1, 0, 1))
-COLD_GROUPS = 2
+COLD_GROUPS = 1
 LATE_GROUPS = 3
 
 FLOPS = 2 * BATCH * K * GATES * UNITS + 2 * BATCH * UNITS * GATES * UNITS
@@ -107,10 +107,10 @@ def tile_hyperlstmcell_pa_t_kernel(
 
         wih_rows = const.tile([P, GATES * K], BF16)
 
-        def load_weights():
+        def load_weights(pair):
             nc.sync.dma_start(
-                out=wih_rows[:].rearrange("p (g k) -> p g k", g=GATES),
-                in_=hc_Wih.rearrange("(g p) k -> p g k", p=P),
+                out=wih_rows[:, 2 * pair * K : (2 * pair + 2) * K].rearrange("p (g k) -> p g k", g=2),
+                in_=hc_Wih.rearrange("(g p) k -> p g k", p=P)[:, 2 * pair : 2 * pair + 2, :],
             )
 
         def load(group):
@@ -119,17 +119,19 @@ def tile_hyperlstmcell_pa_t_kernel(
             kept = kept_tiles[group]
             u_sb = work.tile([P, TILES * K], BF16, bufs=LOADS_AHEAD)
             hyper_h_sb = work.tile([P, COLS], BF16, bufs=LOADS_AHEAD)
-            hyper_c_sb = work.tile([P, COLS], BF16, bufs=LOADS_AHEAD + 4)
+            hyper_c_sb = work.tile([P, COLS], BF16, bufs=LOADS_AHEAD)
             u_parts = u_sb[:].rearrange("p (t s k) -> p t s k", t=TILES, s=2)
             wide = slice(group * TILES * IN, (group + 1) * TILES * IN)
             narrow = slice(group * COLS, (group + 1) * COLS)
             kept["u_sb"] = u_sb
             kept["hyper_h_sb"] = hyper_h_sb
             kept["hyper_c_sb"] = hyper_c_sb
+            if group == 0:
+                load_weights(0)
             nc.sync.dma_start(out=u_parts[:, :, 0, :], in_=x_rows[:, wide].rearrange("p (t k) -> p t k", t=TILES))
             nc.sync.dma_start(out=u_parts[:, :, 1, :], in_=h_rows[:, wide].rearrange("p (t k) -> p t k", t=TILES))
             if group == 0:
-                load_weights()
+                load_weights(1)
             nc.sync.dma_start(out=hyper_h_sb[:], in_=hyper_h_rows[:, narrow])
             nc.sync.dma_start(out=hyper_c_sb[:], in_=hyper_c_rows[:, narrow])
 
@@ -153,6 +155,7 @@ def tile_hyperlstmcell_pa_t_kernel(
         )
         load(1)
         load(2)
+        load(3)
 
         ident_f32 = const.tile([P, P], F32)
         make_identity(nc, ident_f32[:])
@@ -198,7 +201,7 @@ def tile_hyperlstmcell_pa_t_kernel(
             nc.vector.tensor_copy(out=whh_t[:], in_=whh_t_ps[:])
 
         def spread_cell_vectors():
-            cell_ps = psum_v.tile([P, 2, UNITS], F32, tag="v")
+            cell_ps = psum_norm.tile([P, 2, UNITS], F32, tag="norm")
             for c in range(2):
                 col = cols[:, 3 * GATES + c : 3 * GATES + c + 1]
                 nc.tensor.transpose(cell_ps[:, c, :], col.to_broadcast([P, P]), ident_f32[:])
@@ -209,8 +212,9 @@ def tile_hyperlstmcell_pa_t_kernel(
                 return
             kept = kept_tiles[group]
             u_words = kept["u_sb"][:].bitcast(F32)
+            pool, tag = (psum_back, "back") if group == 1 else (psum_in, "in")
             kept["u_t"] = transpose_words(
-                nc, psum_in, "in", ident_f32[:], [u_words[:, t * WORDS : (t + 1) * WORDS] for t in range(TILES)]
+                nc, pool, tag, ident_f32[:], [u_words[:, t * WORDS : (t + 1) * WORDS] for t in range(TILES)]
             )
 
         def copy_u(group):
@@ -235,7 +239,8 @@ def tile_hyperlstmcell_pa_t_kernel(
             if outside(group):
                 return
             kept = kept_tiles[group]
-            mx = psum_mx.tile([P, 2, COLS], F32)
+            pool, tag = (psum_norm, "norm") if group == 0 and pair == 1 else (psum_mx, "mx")
+            mx = pool.tile([P, 2, COLS], F32, tag=tag)
             for e in (0, 1) if group < COLD_GROUPS else MX_ORDER[pair]:
                 g = 2 * pair + e
                 nc.tensor.matmul_mx(
@@ -249,7 +254,7 @@ def tile_hyperlstmcell_pa_t_kernel(
                 )
             kept["mx", pair] = mx
 
-        def add_bias(group, pair):
+        def add_bias(group, pair, on_vector=False):
             if outside(group):
                 return
             kept = kept_tiles[group]
@@ -258,51 +263,34 @@ def tile_hyperlstmcell_pa_t_kernel(
                 kept["mx_bias"] = mx_bias
             for e in range(2):
                 g = 2 * pair + e
-                nc.scalar.activation(
-                    out=kept["mx_bias"][:, g, :],
-                    in_=kept["mx", pair][:, e, :],
-                    func=ACT.Identity,
-                    bias=cols[:, 2 * GATES + g : 2 * GATES + g + 1],
-                )
+                bias = cols[:, 2 * GATES + g : 2 * GATES + g + 1]
+                out = kept["mx_bias"][:, g, :]
+                in_ = kept["mx", pair][:, e, :]
+                if on_vector:
+                    nc.vector.tensor_scalar_add(out=out, in0=in_, scalar1=bias)
+                else:
+                    nc.scalar.activation(out=out, in_=in_, func=ACT.Identity, bias=bias)
 
-        def transpose_hyper_h(group):
-            if outside(group):
-                return
-            states = new_states(group)
-            hyper_h_ps = states[:, COLS:].bitcast(BF16)
-            for t in range(TILES):
-                part = slice(t * P, (t + 1) * P)
-                nc.tensor.transpose(hyper_h_ps[:, part], kept_tiles[group]["hyper_h_sb"][:, part], ident_bf16[:])
-            kept_tiles[group]["hyper_h_ps"] = hyper_h_ps
-
-        def new_states(group):
-            states = psum_in.tile([P, COLS + COLS // 2], F32, tag="in")
-            if not outside(group):
-                kept_tiles[group]["states"] = states
-            return states
-
-        def transpose_hyper_c(group, early):
-            if outside(group):
-                return
-            states = new_states(early) if outside(early) else kept_tiles[early]["states"]
-            for t in range(TILES):
-                part = slice(t * P, (t + 1) * P)
-                nc.tensor.matmul(
-                    out=states[:, part],
-                    lhsT=kept_tiles[group]["hyper_c_sb"][:, part],
-                    rhs=ident_bf16[:],
-                    start=True,
-                    stop=True,
-                )
-            kept_tiles[group]["hyper_c_ps"] = states[:, 0:COLS]
-
-        def copy_hyper_h(group):
+        def transpose_states(group):
             if outside(group):
                 return
             kept = kept_tiles[group]
-            hyper_h_t = work.tile([P, COLS], BF16)
-            nc.scalar.copy(out=hyper_h_t[:], in_=kept["hyper_h_ps"])
-            kept["hyper_h_t"] = hyper_h_t
+            pool, tag = {1: (psum_back, "back"), 2: (psum_norm, "norm")}.get(group, (psum_in, "in"))
+            states = pool.tile([P, 2, COLS], BF16, tag=tag)
+            for t in range(TILES):
+                part = slice(t * P, (t + 1) * P)
+                nc.tensor.transpose(states[:, 0, part], kept["hyper_h_sb"][:, part], ident_bf16[:])
+                nc.tensor.transpose(states[:, 1, part], kept["hyper_c_sb"][:, part], ident_bf16[:])
+            kept["states"] = states
+
+        def copy_states(group):
+            if outside(group):
+                return
+            kept = kept_tiles[group]
+            states_t = work.tile([P, 2, COLS], BF16, bufs=6)
+            nc.scalar.copy(out=states_t[:], in_=kept["states"][:])
+            kept["hyper_h_t"] = states_t[:, 0, :]
+            kept["hyper_c_t"] = states_t[:, 1, :]
 
         def plain_product(group, t):
             if outside(group):
@@ -433,10 +421,8 @@ def tile_hyperlstmcell_pa_t_kernel(
             if outside(group):
                 return
             kept = kept_tiles[group]
-            if pair and group >= N_GROUPS - 2:
-                norm = psum_v.tile([P, 2, TILES, P], F32, tag="v")
-            else:
-                norm = psum_norm.tile([P, 2, TILES, P], F32)
+            pool, tag = (psum_mx, "mx") if pair and group >= N_GROUPS - LATE_GROUPS else (psum_norm, "norm")
+            norm = pool.tile([P, 2, TILES, P], F32, tag=tag)
             for e in range(2):
                 for t in range(TILES):
                     nc.tensor.transpose(norm[:, e, t, :], kept["normed"][:, t, 2 * pair + e, :], ident_f32[:])
@@ -463,7 +449,7 @@ def tile_hyperlstmcell_pa_t_kernel(
                 return
             kept = kept_tiles[group]
             old = work.tile([P, COLS], F32)
-            nc.vector.tensor_tensor(out=old[:], in0=kept["gate", FORGET][:], in1=kept["hyper_c_ps"], op=ALU.mult)
+            nc.vector.tensor_tensor(out=old[:], in0=kept["gate", FORGET][:], in1=kept["hyper_c_t"], op=ALU.mult)
             kept["old"] = old
 
         def new_part(group):
@@ -471,7 +457,7 @@ def tile_hyperlstmcell_pa_t_kernel(
                 return
             kept = kept_tiles[group]
             new = work.tile([P, COLS], F32)
-            nc.gpsimd.tensor_tensor(out=new[:], in0=kept["gate", INPUT][:], in1=kept["gate", CELL][:], op=ALU.mult)
+            nc.vector.tensor_tensor(out=new[:], in0=kept["gate", INPUT][:], in1=kept["gate", CELL][:], op=ALU.mult)
             kept["new"] = new
 
         def transpose_rows(out, tiles):
@@ -498,7 +484,7 @@ def tile_hyperlstmcell_pa_t_kernel(
             has_gate = 0 <= gate_group < N_GROUPS - LATE_GROUPS
             if not has_cell and not has_gate:
                 return
-            back = psum_back.tile([P, 2, TILES, UNITS], F32)
+            back = psum_back.tile([P, 2, TILES, UNITS], F32, tag="back")
             if has_gate:
                 transpose_rows(back[:, 1, :, :], [kept_tiles[gate_group]["gate", OUTPUT]])
                 kept_tiles[gate_group]["gate_o_rows"] = back[:, 1, :, :]
@@ -567,67 +553,96 @@ def tile_hyperlstmcell_pa_t_kernel(
             nc.sync.dma_start(out=new_h_rows[:, group * COLS : (group + 1) * COLS], in_=new_h[:])
 
         def head():
-            transpose_u(0)
-            copy_u(0)
             wih_first = transpose_wih(0)
-            quantise(0)
+            transpose_u(0)
             quantise_wih(nc.vector.tensor_copy, 0, wih_first)
+            copy_u(0)
             wih_second = transpose_wih(1)
-            quantise_wih(nc.scalar.copy, 1, wih_second)
+            quantise(0)
             vector_columns()
+            transpose_states(0)
+            quantise_wih(nc.scalar.copy, 1, wih_second)
+            mx_product(0, 0)
+            copy_states(0)
             transpose_whh()
-
+            transpose_u(1)
+            mx_product(0, 1)
+            add_bias(0, 0)
+            copy_u(1)
+            add_bias(0, 1, on_vector=True)
+            quantise(1)
 
         with tc.manual_schedule():
             head()
-            for i in range(-1, N_GROUPS + 3):
-                if i == 0:
+            for i in range(0, N_GROUPS + 2):
+                if i == 1:
                     spread_cell_vectors()
                 load(i + 4)
                 new_moments(i)
-                transpose_u(i + 2)
-                copy_u(i + 2)
-                transpose_normed(i - 2, 0)
-                cell_moments(i - 4)
-                cell_centre(i - 4)
-                hidden_out(i - 6)
                 plain_product(i, 0)
                 plain_product(i, 1)
                 mx_product(i + 1, 0)
-                activate(i - 2, 0)
+                activate(i - 3, 1)
+                cell_moments(i - 4)
+                hidden_out(i - 6)
+                cell_centre(i - 4)
+                new_part(i - 3)
+                if i > 0:
+                    copy_u(i + 2)
                 add_mx_product(i, 0)
                 add_mx_product(i, 1)
-                transpose_hyper_h(i + 1)
-                transpose_hyper_c(i - 2, i + 1)
-                add_bias(i + 1, 0)
-                copy_hyper_h(i + 1)
-                new_part(i - 3)
-                gate_moments(i, 0)
-                quantise(i + 2)
+                if i == 0:
+                    transpose_u(2)
+                    transpose_states(1)
                 std_eps(i - 1)
-                gate_moments(i, 1)
                 inv_std(i - 1)
-                transpose_normed(i - 2, 1)
-                activate(i - 2, 1)
-                old_part(i - 2)
                 gate_shift(i - 1)
+                add_bias(i + 1, 0)
+                if i == 0:
+                    copy_u(2)
+                    copy_states(1)
+                gate_moments(i, 0)
+                gate_moments(i, 1)
+                transpose_states(i + 2)
+                transpose_normed(i - 2, 0)
+                if i >= N_GROUPS:
+                    activate(i - 2, 0)
                 normalise_on_scalar(i - 1)
+                copy_states(i + 2)
                 normalise_on_vector(i - 1)
                 roots(i)
+                if i < N_GROUPS:
+                    activate(i - 2, 0)
                 mx_product(i + 1, 1)
-                add_bias(i + 1, 1)
                 cell_out(i - 5)
+                quantise(i + 2)
+                add_bias(i + 1, 1)
+                old_part(i - 2)
                 cell_tanh(i - 5)
                 transpose_back(i - 3, i - 5)
+                transpose_normed(i - 2, 1)
+                transpose_u(i + 3)
             last = N_GROUPS - 1
+            new_moments(last - 1 + CELL_LAG)
             new_moments(last + CELL_LAG)
-            std_eps(last - 1 + CELL_LAG)
+            activate(last, 1)
+            cell_moments(last - 1)
+            roots(last - 1 + CELL_LAG)
+            hidden_out(last - 3)
+            cell_centre(last - 1)
+            std_eps(last - 2 + CELL_LAG)
+            new_part(last)
+            inv_std(last - 2 + CELL_LAG)
+            transpose_back(last, -1)
+            cell_out(last - 2)
+            cell_tanh(last - 2)
             cell_moments(last)
-            inv_std(last - 1 + CELL_LAG)
             roots(last + CELL_LAG)
+            std_eps(last - 1 + CELL_LAG)
             cell_centre(last)
-            cell_out(last - 1)
+            inv_std(last - 1 + CELL_LAG)
             hidden_out(last - 2)
+            cell_out(last - 1)
             cell_tanh(last - 1)
             std_eps(last + CELL_LAG)
             inv_std(last + CELL_LAG)

@@ -34,8 +34,7 @@ ROUND_STATS = GATE_STATS + TILES
 
 LOADS_AHEAD = 6
 
-SCALAR_GATES = 3
-
+SCALAR_PAIRS = 4
 MX_ORDER = ((0, 1), (0, 1, 0, 1))
 COLD_GROUPS = 1
 LATE_GROUPS = 3
@@ -280,7 +279,9 @@ def tile_hyperlstmcell_pa_t_kernel(
             for t in range(TILES):
                 part = slice(t * P, (t + 1) * P)
                 nc.tensor.transpose(states[:, 0, part], kept["hyper_h_sb"][:, part], ident_bf16[:])
-                nc.tensor.transpose(states[:, 1, part], kept["hyper_c_sb"][:, part], ident_bf16[:])
+                nc.tensor.matmul(
+                    out=states[:, 1, part], lhsT=kept["hyper_c_sb"][:, part], rhs=ident_bf16[:], start=True, stop=True
+                )
             kept["states"] = states
 
         def copy_states(group):
@@ -376,12 +377,12 @@ def tile_hyperlstmcell_pa_t_kernel(
         def gate_shift(group):
             if outside(group):
                 return
-            shift = work.tile([P, SCALAR_GATES], F32)
+            shift = work.tile([P, SCALAR_PAIRS], F32)
             nc.vector.scalar_tensor_tensor(
                 out=shift[:],
-                in0=shared_tiles[group]["moments"][:, 0:SCALAR_GATES, 1],
+                in0=shared_tiles[group]["moments"][:, 0:SCALAR_PAIRS, 1],
                 scalar=-1.0,
-                in1=shared_tiles[group]["inv"][:, 0:SCALAR_GATES],
+                in1=shared_tiles[group]["inv"][:, 0:SCALAR_PAIRS],
                 op0=ALU.mult,
                 op1=ALU.mult,
             )
@@ -392,13 +393,14 @@ def tile_hyperlstmcell_pa_t_kernel(
                 return
             kept = kept_tiles[group]
             normed = work.tile([P, TILES, GATES, UNITS], F32)
-            for g in range(SCALAR_GATES):
+            for s in range(SCALAR_PAIRS):
+                t, g = divmod(s, GATES)
                 nc.scalar.activation(
-                    out=normed[:, 0, g, :],
-                    in_=kept["v", 0][:, g, :],
+                    out=normed[:, t, g, :],
+                    in_=kept["v", t][:, g, :],
                     func=ACT.Identity,
-                    scale=shared_tiles[group]["inv"][:, g : g + 1],
-                    bias=kept["shift"][:, g : g + 1],
+                    scale=shared_tiles[group]["inv"][:, s : s + 1],
+                    bias=kept["shift"][:, s : s + 1],
                 )
             kept["normed"] = normed
 
@@ -406,8 +408,8 @@ def tile_hyperlstmcell_pa_t_kernel(
             if outside(group):
                 return
             kept = kept_tiles[group]
-            for t, g in [(1, g) for g in range(GATES)] + [(0, g) for g in range(SCALAR_GATES, GATES)]:
-                s = t * GATES + g
+            for s in reversed(range(SCALAR_PAIRS, GATE_STATS)):
+                t, g = divmod(s, GATES)
                 nc.vector.tensor_scalar(
                     out=kept["normed"][:, t, g, :],
                     in0=kept["v", t][:, g, :],
@@ -421,7 +423,9 @@ def tile_hyperlstmcell_pa_t_kernel(
             if outside(group):
                 return
             kept = kept_tiles[group]
-            pool, tag = (psum_mx, "mx") if pair and group >= N_GROUPS - LATE_GROUPS else (psum_norm, "norm")
+            pool, tag = (psum_norm, "norm")
+            if pair and group >= N_GROUPS - LATE_GROUPS:
+                pool, tag = ((psum_mx, "mx"), (psum_in, "in"))[group % 2]
             norm = pool.tile([P, 2, TILES, P], F32, tag=tag)
             for e in range(2):
                 for t in range(TILES):
@@ -574,7 +578,7 @@ def tile_hyperlstmcell_pa_t_kernel(
 
         with tc.manual_schedule():
             head()
-            for i in range(0, N_GROUPS + 2):
+            for i in range(0, N_GROUPS):
                 if i == 1:
                     spread_cell_vectors()
                 load(i + 4)
@@ -604,15 +608,12 @@ def tile_hyperlstmcell_pa_t_kernel(
                 gate_moments(i, 0)
                 gate_moments(i, 1)
                 transpose_states(i + 2)
-                transpose_normed(i - 2, 0)
-                if i >= N_GROUPS:
-                    activate(i - 2, 0)
                 normalise_on_scalar(i - 1)
                 copy_states(i + 2)
+                transpose_normed(i - 2, 0)
                 normalise_on_vector(i - 1)
                 roots(i)
-                if i < N_GROUPS:
-                    activate(i - 2, 0)
+                activate(i - 2, 0)
                 mx_product(i + 1, 1)
                 cell_out(i - 5)
                 quantise(i + 2)
@@ -622,31 +623,64 @@ def tile_hyperlstmcell_pa_t_kernel(
                 transpose_back(i - 3, i - 5)
                 transpose_normed(i - 2, 1)
                 transpose_u(i + 3)
-            last = N_GROUPS - 1
-            new_moments(last - 1 + CELL_LAG)
-            new_moments(last + CELL_LAG)
-            activate(last, 1)
-            cell_moments(last - 1)
-            roots(last - 1 + CELL_LAG)
-            hidden_out(last - 3)
-            cell_centre(last - 1)
-            std_eps(last - 2 + CELL_LAG)
-            new_part(last)
-            inv_std(last - 2 + CELL_LAG)
-            transpose_back(last, -1)
-            cell_out(last - 2)
-            cell_tanh(last - 2)
-            cell_moments(last)
-            roots(last + CELL_LAG)
-            std_eps(last - 1 + CELL_LAG)
-            cell_centre(last)
-            inv_std(last - 1 + CELL_LAG)
-            hidden_out(last - 2)
-            cell_out(last - 1)
-            cell_tanh(last - 1)
-            std_eps(last + CELL_LAG)
-            inv_std(last + CELL_LAG)
-            hidden_out(last - 1)
-            cell_out(last)
-            cell_tanh(last)
-            hidden_out(last)
+            end = N_GROUPS
+            for r in range(end, end + CELL_LAG):
+                new_moments(r)
+            transpose_normed(end - 2, 0)
+            activate(end - 3, 1)
+            transpose_normed(end - 2, 1)
+            cell_moments(end - 4)
+            hidden_out(end - 6)
+            cell_centre(end - 4)
+            new_part(end - 3)
+            std_eps(end - 1)
+            inv_std(end - 1)
+            gate_shift(end - 1)
+            activate(end - 2, 0)
+            normalise_on_scalar(end - 1)
+            normalise_on_vector(end - 1)
+            roots(end)
+            transpose_back(end - 3, end - 5)
+            activate(end - 2, 1)
+            old_part(end - 2)
+            transpose_normed(end - 1, 0)
+            transpose_normed(end - 1, 1)
+            cell_out(end - 5)
+            new_part(end - 2)
+            cell_tanh(end - 5)
+            transpose_back(end - 2, -1)
+            cell_moments(end - 3)
+            std_eps(end)
+            cell_centre(end - 3)
+            inv_std(end)
+            roots(end + 1)
+            activate(end - 1, 0)
+            activate(end - 1, 1)
+            hidden_out(end - 5)
+            cell_out(end - 4)
+            old_part(end - 1)
+            new_part(end - 1)
+            cell_tanh(end - 4)
+            transpose_back(end - 1, end - 4)
+            cell_moments(end - 2)
+            roots(end + 2)
+            std_eps(end + 1)
+            cell_centre(end - 2)
+            inv_std(end + 1)
+            cell_out(end - 3)
+            cell_tanh(end - 3)
+            cell_moments(end - 1)
+            roots(end + 3)
+            hidden_out(end - 4)
+            std_eps(end + 2)
+            cell_centre(end - 1)
+            inv_std(end + 2)
+            cell_out(end - 2)
+            hidden_out(end - 3)
+            cell_tanh(end - 2)
+            std_eps(end + 3)
+            hidden_out(end - 2)
+            inv_std(end + 3)
+            cell_out(end - 1)
+            cell_tanh(end - 1)
+            hidden_out(end - 1)

@@ -34,7 +34,7 @@ ROUND_STATS = GATE_STATS + TILES
 
 LOADS_AHEAD = 6
 
-SCALAR_PAIRS = 4
+SCALAR_PAIRS = 3
 MX_ORDER = ((0, 1), (0, 1, 0, 1))
 COLD_GROUPS = 1
 LATE_GROUPS = 3
@@ -279,6 +279,8 @@ def tile_hyperlstmcell_pa_t_kernel(
             for t in range(TILES):
                 part = slice(t * P, (t + 1) * P)
                 nc.tensor.transpose(states[:, 0, part], kept["hyper_h_sb"][:, part], ident_bf16[:])
+            for t in range(TILES):
+                part = slice(t * P, (t + 1) * P)
                 nc.tensor.matmul(
                     out=states[:, 1, part], lhsT=kept["hyper_c_sb"][:, part], rhs=ident_bf16[:], start=True, stop=True
                 )
@@ -607,13 +609,13 @@ def tile_hyperlstmcell_pa_t_kernel(
                     copy_states(1)
                 gate_moments(i, 0)
                 gate_moments(i, 1)
-                transpose_states(i + 2)
                 normalise_on_scalar(i - 1)
-                copy_states(i + 2)
                 transpose_normed(i - 2, 0)
+                transpose_states(i + 2)
                 normalise_on_vector(i - 1)
                 roots(i)
                 activate(i - 2, 0)
+                copy_states(i + 2)
                 mx_product(i + 1, 1)
                 cell_out(i - 5)
                 quantise(i + 2)

@@ -36,7 +36,7 @@ LOADS_AHEAD = 6
 
 SCALAR_PAIRS = 3
 MX_ORDER = ((0, 1), (0, 1, 0, 1))
-COLD_GROUPS = 1
+COLD_GROUPS = 2
 LATE_GROUPS = 3
 
 FLOPS = 2 * BATCH * K * GATES * UNITS + 2 * BATCH * UNITS * GATES * UNITS
@@ -329,11 +329,11 @@ def tile_hyperlstmcell_pa_t_kernel(
             moments = work.tile([P, ROUND_STATS, 3], F32, bufs=4)
             shared_tiles[r]["moments"] = moments
 
-        def gate_moments(group, t):
+        def gate_moments(group, t, pairs=(0, 1)):
             if outside(group):
                 return
             moments = shared_tiles[group]["moments"]
-            for pair in range(GATES // 2):
+            for pair in pairs:
                 first = t * GATES + 2 * pair
                 nc.vector.bn_stats(
                     out=moments[:, first : first + 2, :].rearrange("p s m -> p (s m)"),
@@ -379,6 +379,8 @@ def tile_hyperlstmcell_pa_t_kernel(
         def gate_shift(group):
             if outside(group):
                 return
+            normed = work.tile([P, TILES, GATES, UNITS], F32)
+            kept_tiles[group]["normed"] = normed
             shift = work.tile([P, SCALAR_PAIRS], F32)
             nc.vector.scalar_tensor_tensor(
                 out=shift[:],
@@ -394,23 +396,21 @@ def tile_hyperlstmcell_pa_t_kernel(
             if outside(group):
                 return
             kept = kept_tiles[group]
-            normed = work.tile([P, TILES, GATES, UNITS], F32)
             for s in range(SCALAR_PAIRS):
                 t, g = divmod(s, GATES)
                 nc.scalar.activation(
-                    out=normed[:, t, g, :],
+                    out=kept["normed"][:, t, g, :],
                     in_=kept["v", t][:, g, :],
                     func=ACT.Identity,
                     scale=shared_tiles[group]["inv"][:, s : s + 1],
                     bias=kept["shift"][:, s : s + 1],
                 )
-            kept["normed"] = normed
 
         def normalise_on_vector(group):
             if outside(group):
                 return
             kept = kept_tiles[group]
-            for s in reversed(range(SCALAR_PAIRS, GATE_STATS)):
+            for s in range(SCALAR_PAIRS, GATE_STATS):
                 t, g = divmod(s, GATES)
                 nc.vector.tensor_scalar(
                     out=kept["normed"][:, t, g, :],
@@ -466,6 +466,14 @@ def tile_hyperlstmcell_pa_t_kernel(
             nc.vector.tensor_tensor(out=new[:], in0=kept["gate", INPUT][:], in1=kept["gate", CELL][:], op=ALU.mult)
             kept["new"] = new
 
+        def cell_sum(group):
+            if outside(group):
+                return
+            kept = kept_tiles[group]
+            raw = work.tile([P, COLS], F32)
+            nc.vector.tensor_tensor(out=raw[:], in0=kept["old"][:], in1=kept["new"][:], op=ALU.add)
+            kept["raw"] = raw
+
         def transpose_rows(out, tiles):
             for t in range(TILES):
                 for n, tile in enumerate(tiles):
@@ -495,7 +503,7 @@ def tile_hyperlstmcell_pa_t_kernel(
                 transpose_rows(back[:, 1, :, :], [kept_tiles[gate_group]["gate", OUTPUT]])
                 kept_tiles[gate_group]["gate_o_rows"] = back[:, 1, :, :]
             if has_cell:
-                transpose_rows(back[:, 0, :, :], [kept_tiles[cell_group]["old"], kept_tiles[cell_group]["new"]])
+                transpose_rows(back[:, 0, :, :], [kept_tiles[cell_group]["raw"]])
                 kept_tiles[cell_group]["raw_c"] = back[:, 0, :, :]
 
         def cell_moments(group):
@@ -585,14 +593,14 @@ def tile_hyperlstmcell_pa_t_kernel(
                     spread_cell_vectors()
                 load(i + 4)
                 new_moments(i)
-                plain_product(i, 0)
                 plain_product(i, 1)
+                plain_product(i, 0)
                 mx_product(i + 1, 0)
                 activate(i - 3, 1)
                 cell_moments(i - 4)
-                hidden_out(i - 6)
-                cell_centre(i - 4)
                 new_part(i - 3)
+                cell_centre(i - 4)
+                cell_sum(i - 3)
                 if i > 0:
                     copy_u(i + 2)
                 add_mx_product(i, 0)
@@ -600,28 +608,30 @@ def tile_hyperlstmcell_pa_t_kernel(
                 if i == 0:
                     transpose_u(2)
                     transpose_states(1)
-                std_eps(i - 1)
-                inv_std(i - 1)
-                gate_shift(i - 1)
                 add_bias(i + 1, 0)
                 if i == 0:
                     copy_u(2)
                     copy_states(1)
+                cell_tanh(i - 6)
                 gate_moments(i, 0)
-                gate_moments(i, 1)
-                normalise_on_scalar(i - 1)
+                std_eps(i - 1)
+                hidden_out(i - 6)
+                gate_moments(i, 1, (0,))
+                inv_std(i - 1)
+                gate_moments(i, 1, (1,))
+                roots(i)
+                gate_shift(i - 1)
                 transpose_normed(i - 2, 0)
                 transpose_states(i + 2)
                 normalise_on_vector(i - 1)
-                roots(i)
                 activate(i - 2, 0)
                 copy_states(i + 2)
                 mx_product(i + 1, 1)
                 cell_out(i - 5)
                 quantise(i + 2)
                 add_bias(i + 1, 1)
+                normalise_on_scalar(i - 1)
                 old_part(i - 2)
-                cell_tanh(i - 5)
                 transpose_back(i - 3, i - 5)
                 transpose_normed(i - 2, 1)
                 transpose_u(i + 3)
@@ -630,59 +640,60 @@ def tile_hyperlstmcell_pa_t_kernel(
                 new_moments(r)
             transpose_normed(end - 2, 0)
             activate(end - 3, 1)
+            cell_tanh(end - 6)
             transpose_normed(end - 2, 1)
             cell_moments(end - 4)
-            hidden_out(end - 6)
-            cell_centre(end - 4)
             new_part(end - 3)
             std_eps(end - 1)
+            cell_centre(end - 4)
             inv_std(end - 1)
+            hidden_out(end - 6)
             gate_shift(end - 1)
+            transpose_back(end - 3, end - 5)
+            normalise_on_vector(end - 1)
             activate(end - 2, 0)
             normalise_on_scalar(end - 1)
-            normalise_on_vector(end - 1)
             roots(end)
-            transpose_back(end - 3, end - 5)
             activate(end - 2, 1)
+            cell_out(end - 5)
+            cell_moments(end - 3)
+            roots(end + 1)
             old_part(end - 2)
+            cell_centre(end - 3)
+            new_part(end - 2)
             transpose_normed(end - 1, 0)
             transpose_normed(end - 1, 1)
-            cell_out(end - 5)
-            new_part(end - 2)
-            cell_tanh(end - 5)
             transpose_back(end - 2, -1)
-            cell_moments(end - 3)
-            std_eps(end)
-            cell_centre(end - 3)
-            inv_std(end)
-            roots(end + 1)
             activate(end - 1, 0)
             activate(end - 1, 1)
-            hidden_out(end - 5)
-            cell_out(end - 4)
+            cell_tanh(end - 5)
+            std_eps(end)
+            cell_moments(end - 2)
+            inv_std(end)
+            roots(end + 2)
             old_part(end - 1)
+            cell_out(end - 4)
             new_part(end - 1)
+            hidden_out(end - 5)
             cell_tanh(end - 4)
             transpose_back(end - 1, end - 4)
-            cell_moments(end - 2)
-            roots(end + 2)
-            std_eps(end + 1)
             cell_centre(end - 2)
+            std_eps(end + 1)
+            cell_moments(end - 1)
             inv_std(end + 1)
+            roots(end + 3)
+            cell_centre(end - 1)
             cell_out(end - 3)
             cell_tanh(end - 3)
-            cell_moments(end - 1)
-            roots(end + 3)
             hidden_out(end - 4)
             std_eps(end + 2)
-            cell_centre(end - 1)
+            hidden_out(end - 3)
             inv_std(end + 2)
             cell_out(end - 2)
-            hidden_out(end - 3)
             cell_tanh(end - 2)
             std_eps(end + 3)
-            hidden_out(end - 2)
             inv_std(end + 3)
             cell_out(end - 1)
             cell_tanh(end - 1)
+            hidden_out(end - 2)
             hidden_out(end - 1)

@@ -466,14 +466,6 @@ def tile_hyperlstmcell_pa_t_kernel(
             nc.vector.tensor_tensor(out=new[:], in0=kept["gate", INPUT][:], in1=kept["gate", CELL][:], op=ALU.mult)
             kept["new"] = new
 
-        def cell_sum(group):
-            if outside(group):
-                return
-            kept = kept_tiles[group]
-            raw = work.tile([P, COLS], F32)
-            nc.vector.tensor_tensor(out=raw[:], in0=kept["old"][:], in1=kept["new"][:], op=ALU.add)
-            kept["raw"] = raw
-
         def transpose_rows(out, tiles):
             for t in range(TILES):
                 for n, tile in enumerate(tiles):
@@ -503,7 +495,7 @@ def tile_hyperlstmcell_pa_t_kernel(
                 transpose_rows(back[:, 1, :, :], [kept_tiles[gate_group]["gate", OUTPUT]])
                 kept_tiles[gate_group]["gate_o_rows"] = back[:, 1, :, :]
             if has_cell:
-                transpose_rows(back[:, 0, :, :], [kept_tiles[cell_group]["raw"]])
+                transpose_rows(back[:, 0, :, :], [kept_tiles[cell_group]["old"], kept_tiles[cell_group]["new"]])
                 kept_tiles[cell_group]["raw_c"] = back[:, 0, :, :]
 
         def cell_moments(group):
@@ -600,7 +592,6 @@ def tile_hyperlstmcell_pa_t_kernel(
                 cell_moments(i - 4)
                 new_part(i - 3)
                 cell_centre(i - 4)
-                cell_sum(i - 3)
                 if i > 0:
                     copy_u(i + 2)
                 add_mx_product(i, 0)
@@ -627,8 +618,8 @@ def tile_hyperlstmcell_pa_t_kernel(
                 activate(i - 2, 0)
                 copy_states(i + 2)
                 mx_product(i + 1, 1)
-                cell_out(i - 5)
                 quantise(i + 2)
+                cell_out(i - 5)
                 add_bias(i + 1, 1)
                 normalise_on_scalar(i - 1)
                 old_part(i - 2)
@@ -644,26 +635,26 @@ def tile_hyperlstmcell_pa_t_kernel(
             transpose_normed(end - 2, 1)
             cell_moments(end - 4)
             new_part(end - 3)
-            std_eps(end - 1)
+            activate(end - 2, 0)
             cell_centre(end - 4)
-            inv_std(end - 1)
+            activate(end - 2, 1)
+            old_part(end - 2)
+            std_eps(end - 1)
             hidden_out(end - 6)
+            inv_std(end - 1)
+            new_part(end - 2)
             gate_shift(end - 1)
             transpose_back(end - 3, end - 5)
             normalise_on_vector(end - 1)
-            activate(end - 2, 0)
             normalise_on_scalar(end - 1)
             roots(end)
-            activate(end - 2, 1)
-            cell_out(end - 5)
-            cell_moments(end - 3)
-            roots(end + 1)
-            old_part(end - 2)
-            cell_centre(end - 3)
-            new_part(end - 2)
+            transpose_back(end - 2, -1)
             transpose_normed(end - 1, 0)
             transpose_normed(end - 1, 1)
-            transpose_back(end - 2, -1)
+            cell_moments(end - 3)
+            roots(end + 1)
+            cell_out(end - 5)
+            cell_centre(end - 3)
             activate(end - 1, 0)
             activate(end - 1, 1)
             cell_tanh(end - 5)
@@ -672,12 +663,12 @@ def tile_hyperlstmcell_pa_t_kernel(
             inv_std(end)
             roots(end + 2)
             old_part(end - 1)
-            cell_out(end - 4)
             new_part(end - 1)
+            cell_centre(end - 2)
+            cell_out(end - 4)
             hidden_out(end - 5)
             cell_tanh(end - 4)
             transpose_back(end - 1, end - 4)
-            cell_centre(end - 2)
             std_eps(end + 1)
             cell_moments(end - 1)
             inv_std(end + 1)
@@ -685,10 +676,10 @@ def tile_hyperlstmcell_pa_t_kernel(
             cell_centre(end - 1)
             cell_out(end - 3)
             cell_tanh(end - 3)
-            hidden_out(end - 4)
             std_eps(end + 2)
-            hidden_out(end - 3)
+            hidden_out(end - 4)
             inv_std(end + 2)
+            hidden_out(end - 3)
             cell_out(end - 2)
             cell_tanh(end - 2)
             std_eps(end + 3)

from contextlib import ExitStack

import concourse.mybir as mybir
from concourse.masks import make_identity

F32 = mybir.dt.float32
BF16 = mybir.dt.bfloat16
U32 = mybir.dt.uint32
U8 = mybir.dt.uint8
FP8X4 = mybir.dt.float8_e4m3fn_x4
ALU = mybir.AluOpType
ACT = mybir.ActivationFunctionType

P = 128
BATCH = 4096
IN = 256
K = 2 * IN
UNITS = 128
GATES = 4
EPS = 1e-6

N_TILES = BATCH // P
TILES = 2
N_GROUPS = N_TILES // TILES
COLS = TILES * P
GATE_STATS = TILES * GATES
WORDS = K // 2

GATE_FUNCS = (ACT.Sigmoid, ACT.Sigmoid, ACT.Tanh, ACT.Sigmoid)
INPUT, FORGET, CELL, OUTPUT = range(GATES)

CELL_LAG = 4
ROUND_STATS = GATE_STATS + TILES

LOADS_AHEAD = 6

SCALAR_PAIRS = 3
MX_ORDER = ((0, 1), (0, 1, 0, 1))
COLD_GROUPS = 2
LATE_GROUPS = 3

FLOPS = 2 * BATCH * K * GATES * UNITS + 2 * BATCH * UNITS * GATES * UNITS


def transpose_words(nc, psum, tag, ident_f32, words):
    k_first = psum.tile([P, 2, 2, P], F32, tag=tag)
    for i in range(2):
        for u in range(2):
            nc.tensor.transpose(k_first[:, i, u, :], words[i][:, u::2], ident_f32)
    return k_first


def group_words(copy, k_first, grouped):
    copy(
        out=grouped.bitcast(F32).rearrange("p (i r u) -> p i r u", i=2, u=2),
        in_=k_first[:].rearrange("p i u r -> p i r u"),
    )


def tile_hyperlstmcell_pa_t_kernel(
    tc,
    x,
    h,
    hyper_h,
    hyper_c,
    hc_Wih,
    hc_bih,
    hc_Whh,
    hc_ln_gamma,
    hc_ln_beta,
    hc_lnc_gamma,
    hc_lnc_beta,
    out_0,
    out_1,
):
    nc = tc.nc
    with ExitStack() as ctx:
        const = ctx.enter_context(tc.tile_pool(name="const", bufs=1))
        work = ctx.enter_context(tc.tile_pool(name="work", bufs=2))
        psum_in = ctx.enter_context(tc.psum_pool(name="psum_in", bufs=1))
        psum_mx = ctx.enter_context(tc.psum_pool(name="psum_mx", bufs=1))
        psum_v = ctx.enter_context(tc.psum_pool(name="psum_v", bufs=4))
        psum_norm = ctx.enter_context(tc.psum_pool(name="psum_norm", bufs=1))
        psum_back = ctx.enter_context(tc.psum_pool(name="psum_back", bufs=1))

        x_rows = x.rearrange("(p r) k -> p (r k)", r=N_TILES)
        h_rows = h.rearrange("(p r) k -> p (r k)", r=N_TILES)
        hyper_h_rows = hyper_h.rearrange("(p r) k -> p (r k)", r=N_TILES)
        hyper_c_rows = hyper_c.rearrange("(p r) k -> p (r k)", r=N_TILES)
        new_h_rows = out_0.rearrange("(p r) k -> p (r k)", r=N_TILES)
        new_c_rows = out_1.rearrange("(p r) k -> p (r k)", r=N_TILES)

        kept_tiles = [dict() for group in range(N_GROUPS)]
        shared_tiles = [dict() for r in range(N_GROUPS + CELL_LAG)]

        def outside(group):
            return group < 0 or group >= N_GROUPS

        def no_round(r):
            return r < 0 or r >= N_GROUPS + CELL_LAG

        def live(r):
            first = 0 if r < N_GROUPS else GATE_STATS
            last = ROUND_STATS if r >= CELL_LAG else GATE_STATS
            return slice(first, last)

        wih_rows = const.tile([P, GATES * K], BF16)

        def load_weights(pair):
            nc.sync.dma_start(
                out=wih_rows[:, 2 * pair * K : (2 * pair + 2) * K].rearrange("p (g k) -> p g k", g=2),
                in_=hc_Wih.rearrange("(g p) k -> p g k", p=P)[:, 2 * pair : 2 * pair + 2, :],
            )

        def load(group):
            if outside(group):
                return
            kept = kept_tiles[group]
            u_sb = work.tile([P, TILES * K], BF16, bufs=LOADS_AHEAD)
            hyper_h_sb = work.tile([P, COLS], BF16, bufs=LOADS_AHEAD)
            hyper_c_sb = work.tile([P, COLS], BF16, bufs=LOADS_AHEAD)
            u_parts = u_sb[:].rearrange("p (t s k) -> p t s k", t=TILES, s=2)
            wide = slice(group * TILES * IN, (group + 1) * TILES * IN)
            narrow = slice(group * COLS, (group + 1) * COLS)
            kept["u_sb"] = u_sb
            kept["hyper_h_sb"] = hyper_h_sb
            kept["hyper_c_sb"] = hyper_c_sb
            if group == 0:
                load_weights(0)
            nc.sync.dma_start(out=u_parts[:, :, 0, :], in_=x_rows[:, wide].rearrange("p (t k) -> p t k", t=TILES))
            nc.sync.dma_start(out=u_parts[:, :, 1, :], in_=h_rows[:, wide].rearrange("p (t k) -> p t k", t=TILES))
            if group == 0:
                load_weights(1)
            nc.sync.dma_start(out=hyper_h_sb[:], in_=hyper_h_rows[:, narrow])
            nc.sync.dma_start(out=hyper_c_sb[:], in_=hyper_c_rows[:, narrow])

        half = const.tile([P, ROUND_STATS], F32)
        nc.vector.memset(half[:], 0.5)
        table = const.tile([P, 1], F32)
        nc.scalar.activation(out=table[:], in_=half[:, 0:1], func=ACT.Sigmoid)
        load(0)

        rows = const.tile([P, P], BF16)
        nc.vector.memset(rows[:], 0.0)
        nc.scalar.dma_start(out=rows[2 * GATES : 3 * GATES, :], in_=hc_bih.rearrange("(g j) -> g j", g=GATES))
        nc.scalar.dma_start(out=rows[0:GATES, :], in_=hc_ln_gamma)
        nc.scalar.dma_start(out=rows[GATES : 2 * GATES, :], in_=hc_ln_beta)
        nc.scalar.dma_start(out=rows[3 * GATES : 3 * GATES + 1, :], in_=hc_lnc_gamma.rearrange("(o n) -> o n", o=1))
        nc.scalar.dma_start(out=rows[3 * GATES + 1 : 3 * GATES + 2, :], in_=hc_lnc_beta.rearrange("(o n) -> o n", o=1))
        whh_rows = const.tile([P, GATES * UNITS], BF16)
        nc.sync.dma_start(
            out=whh_rows[:].rearrange("p (g k) -> p g k", g=GATES),
            in_=hc_Whh.rearrange("(g p) k -> p g k", p=P),
        )
        load(1)
        load(2)
        load(3)

        ident_f32 = const.tile([P, P], F32)
        make_identity(nc, ident_f32[:])
        ident_bf16 = const.tile([P, P], BF16)
        nc.vector.tensor_copy(out=ident_bf16[:], in_=ident_f32[:])
        wih_codes = const.tile([P, GATES * P], U32, align_bytes=64)
        wih_scales = const.tile([P, GATES * P], U8, align_bytes=64)
        cols = const.tile([P, 3 * GATES + 2], F32)
        whh_t = const.tile([P, GATES * P], BF16)
        cell_all = const.tile([P, 2, UNITS], F32)
        gamma_c_all = cell_all[:, 0, :]
        beta_c_all = cell_all[:, 1, :]

        def transpose_wih(pair):
            wih_words = wih_rows[:].bitcast(F32)
            return transpose_words(
                nc,
                psum_v,
                "v",
                ident_f32[:],
                [wih_words[:, g * WORDS : (g + 1) * WORDS] for g in (2 * pair, 2 * pair + 1)],
            )

        def quantise_wih(copy, pair, wih_t):
            wih_grouped = const.tile([P, 2 * P * 4], BF16, align_bytes=64, tag="wih_grouped", bufs=2)
            group_words(copy, wih_t, wih_grouped[:])
            part = slice(2 * pair * P, (2 * pair + 2) * P)
            nc.vector.quantize_mx(out=wih_codes[:, part].bitcast(FP8X4), scales=wih_scales[:, part], in_=wih_grouped[:])

        def vector_columns():
            cols_ps = psum_v.tile([P, P], BF16, tag="v")
            nc.tensor.transpose(cols_ps[:], rows[:], ident_bf16[:])
            nc.vector.tensor_copy(out=cols[:], in_=cols_ps[:, 0 : 3 * GATES + 2])
            forget_beta = cols[:, GATES + FORGET : GATES + FORGET + 1]
            nc.vector.tensor_scalar_add(out=forget_beta, in0=forget_beta, scalar1=1.0)

        def transpose_whh():
            whh_t_ps = psum_v.tile([P, GATES * P], BF16, tag="v")
            for g in range(GATES):
                nc.tensor.transpose(
                    whh_t_ps[:, g * P : (g + 1) * P], whh_rows[:, g * UNITS : (g + 1) * UNITS], ident_bf16[:]
                )
            nc.vector.tensor_copy(out=whh_t[:], in_=whh_t_ps[:])

        def spread_cell_vectors():
            cell_ps = psum_norm.tile([P, 2, UNITS], F32, tag="norm")
            for c in range(2):
                col = cols[:, 3 * GATES + c : 3 * GATES + c + 1]
                nc.tensor.transpose(cell_ps[:, c, :], col.to_broadcast([P, P]), ident_f32[:])
            nc.vector.tensor_copy(out=cell_all[:], in_=cell_ps[:])

        def transpose_u(group):
            if outside(group):
                return
            kept = kept_tiles[group]
            u_words = kept["u_sb"][:].bitcast(F32)
            pool, tag = (psum_back, "back") if group == 1 else (psum_in, "in")
            kept["u_t"] = transpose_words(
                nc, pool, tag, ident_f32[:], [u_words[:, t * WORDS : (t + 1) * WORDS] for t in range(TILES)]
            )

        def copy_u(group):
            if outside(group):
                return
            kept = kept_tiles[group]
            u_grouped = work.tile([P, COLS * 4], BF16, align_bytes=64)
            group_words(nc.scalar.copy, kept["u_t"], u_grouped[:])
            kept["u_grouped"] = u_grouped

        def quantise(group):
            if outside(group):
                return
            kept = kept_tiles[group]
            u_codes = work.tile([P, COLS], U32, align_bytes=64)
            u_scales = work.tile([P, COLS], U8, align_bytes=64)
            nc.vector.quantize_mx(out=u_codes[:].bitcast(FP8X4), scales=u_scales[:], in_=kept["u_grouped"][:])
            kept["u_codes"] = u_codes
            kept["u_scales"] = u_scales

        def mx_product(group, pair):
            if outside(group):
                return
            kept = kept_tiles[group]
            pool, tag = (psum_norm, "norm") if group == 0 and pair == 1 else (psum_mx, "mx")
            mx = pool.tile([P, 2, COLS], F32, tag=tag)
            for e in (0, 1) if group < COLD_GROUPS else MX_ORDER[pair]:
                g = 2 * pair + e
                nc.tensor.matmul_mx(
                    out=mx[:, e, :],
                    lhsT=wih_codes[:, g * P : (g + 1) * P].bitcast(FP8X4),
                    lhsT_scale=wih_scales[:, g * P : (g + 1) * P],
                    rhs=kept["u_codes"][:].bitcast(FP8X4),
                    rhs_scale=kept["u_scales"][:],
                    start=True,
                    stop=True,
                )
            kept["mx", pair] = mx

        def add_bias(group, pair, on_vector=False):
            if outside(group):
                return
            kept = kept_tiles[group]
            if pair == 0:
                mx_bias = work.tile([P, GATES, COLS], F32, bufs=3)
                kept["mx_bias"] = mx_bias
            for e in range(2):
                g = 2 * pair + e
                bias = cols[:, 2 * GATES + g : 2 * GATES + g + 1]
                out = kept["mx_bias"][:, g, :]
                in_ = kept["mx", pair][:, e, :]
                if on_vector:
                    nc.vector.tensor_scalar_add(out=out, in0=in_, scalar1=bias)
                else:
                    nc.scalar.activation(out=out, in_=in_, func=ACT.Identity, bias=bias)

        def transpose_states(group):
            if outside(group):
                return
            kept = kept_tiles[group]
            pool, tag = {1: (psum_back, "back"), 2: (psum_norm, "norm")}.get(group, (psum_in, "in"))
            states = pool.tile([P, 2, COLS], BF16, tag=tag)
            for t in range(TILES):
                part = slice(t * P, (t + 1) * P)
                nc.tensor.transpose(states[:, 0, part], kept["hyper_h_sb"][:, part], ident_bf16[:])
            for t in range(TILES):
                part = slice(t * P, (t + 1) * P)
                nc.tensor.matmul(
                    out=states[:, 1, part], lhsT=kept["hyper_c_sb"][:, part], rhs=ident_bf16[:], start=True, stop=True
                )
            kept["states"] = states

        def copy_states(group):
            if outside(group):
                return
            kept = kept_tiles[group]
            states_t = work.tile([P, 2, COLS], BF16, bufs=6)
            nc.scalar.copy(out=states_t[:], in_=kept["states"][:])
            kept["hyper_h_t"] = states_t[:, 0, :]
            kept["hyper_c_t"] = states_t[:, 1, :]

        def plain_product(group, t):
            if outside(group):
                return
            kept = kept_tiles[group]
            v = psum_v.tile([P, GATES, UNITS], F32, tag="v")
            nc.tensor.matmul(
                out=v[:].rearrange("p g j -> p (g j)"),
                lhsT=kept["hyper_h_t"][:, t * P : (t + 1) * P],
                rhs=whh_t[:],
                start=True,
                stop=False,
            )
            kept["v", t] = v

        def add_mx_product(group, t):
            if outside(group):
                return
            kept = kept_tiles[group]
            for g in range(GATES):
                nc.tensor.matmul(
                    out=kept["v", t][:, g, :],
                    lhsT=kept["mx_bias"][:, g, t * P : (t + 1) * P],
                    rhs=ident_f32[:],
                    start=False,
                    stop=g == GATES - 1,
                    is_transpose=True,
                )

        def new_moments(r):
            if no_round(r):
                return
            moments = work.tile([P, ROUND_STATS, 3], F32, bufs=4)
            shared_tiles[r]["moments"] = moments

        def gate_moments(group, t, pairs=(0, 1)):
            if outside(group):
                return
            moments = shared_tiles[group]["moments"]
            for pair in pairs:
                first = t * GATES + 2 * pair
                nc.vector.bn_stats(
                    out=moments[:, first : first + 2, :].rearrange("p s m -> p (s m)"),
                    in_=kept_tiles[group]["v", t][:, 2 * pair : 2 * pair + 2, :].rearrange("p g j -> p j g"),
                )

        def roots(r):
            if no_round(r):
                return
            shared = shared_tiles[r]
            live_cols = live(r)
            root = work.tile([P, ROUND_STATS], F32)
            nc.gpsimd.tensor_tensor(
                out=root[:, live_cols], in0=shared["moments"][:, live_cols, 2], in1=half[:, live_cols], op=ALU.pow
            )
            shared["root"] = root

        def std_eps(r):
            if no_round(r):
                return
            shared = shared_tiles[r]
            live_cols = live(r)
            std = work.tile([P, ROUND_STATS], F32)
            nc.vector.tensor_scalar(
                out=std[:, live_cols],
                in0=shared["root"][:, live_cols],
                scalar1=1.0 / (UNITS - 1) ** 0.5,
                scalar2=EPS,
                op0=ALU.mult,
                op1=ALU.add,
            )
            shared["std"] = std

        def inv_std(r):
            if no_round(r):
                return
            shared = shared_tiles[r]
            live_cols = live(r)
            inv = work.tile([P, ROUND_STATS], F32)
            nc.vector.reciprocal(out=inv[:, live_cols], in_=shared["std"][:, live_cols])
            shared["inv"] = inv

        def gate_shift(group):
            if outside(group):
                return
            normed = work.tile([P, TILES, GATES, UNITS], F32)
            kept_tiles[group]["normed"] = normed
            shift = work.tile([P, SCALAR_PAIRS], F32)
            nc.vector.scalar_tensor_tensor(
                out=shift[:],
                in0=shared_tiles[group]["moments"][:, 0:SCALAR_PAIRS, 1],
                scalar=-1.0,
                in1=shared_tiles[group]["inv"][:, 0:SCALAR_PAIRS],
                op0=ALU.mult,
                op1=ALU.mult,
            )
            kept_tiles[group]["shift"] = shift

        def normalise_on_scalar(group):
            if outside(group):
                return
            kept = kept_tiles[group]
            for s in range(SCALAR_PAIRS):
                t, g = divmod(s, GATES)
                nc.scalar.activation(
                    out=kept["normed"][:, t, g, :],
                    in_=kept["v", t][:, g, :],
                    func=ACT.Identity,
                    scale=shared_tiles[group]["inv"][:, s : s + 1],
                    bias=kept["shift"][:, s : s + 1],
                )

        def normalise_on_vector(group):
            if outside(group):
                return
            kept = kept_tiles[group]
            for s in range(SCALAR_PAIRS, GATE_STATS):
                t, g = divmod(s, GATES)
                nc.vector.tensor_scalar(
                    out=kept["normed"][:, t, g, :],
                    in0=kept["v", t][:, g, :],
                    scalar1=shared_tiles[group]["moments"][:, s, 1:2],
                    scalar2=shared_tiles[group]["inv"][:, s : s + 1],
                    op0=ALU.subtract,
                    op1=ALU.mult,
                )

        def transpose_normed(group, pair):
            if outside(group):
                return
            kept = kept_tiles[group]
            pool, tag = (psum_norm, "norm")
            if pair and group >= N_GROUPS - LATE_GROUPS:
                pool, tag = ((psum_mx, "mx"), (psum_in, "in"))[group % 2]
            norm = pool.tile([P, 2, TILES, P], F32, tag=tag)
            for e in range(2):
                for t in range(TILES):
                    nc.tensor.transpose(norm[:, e, t, :], kept["normed"][:, t, 2 * pair + e, :], ident_f32[:])
            kept["norm", pair] = norm

        def activate(group, pair):
            if outside(group):
                return
            kept = kept_tiles[group]
            for e in range(2):
                g = 2 * pair + e
                gate = work.tile([P, COLS], F32, tag="gate_%d" % g, bufs=6 if g == OUTPUT else 3)
                nc.scalar.activation(
                    out=gate[:],
                    in_=kept["norm", pair][:, e, :, :].rearrange("p t b -> p (t b)"),
                    func=GATE_FUNCS[g],
                    scale=cols[:, g : g + 1],
                    bias=cols[:, GATES + g : GATES + g + 1],
                )
                kept["gate", g] = gate

        def old_part(group):
            if outside(group):
                return
            kept = kept_tiles[group]
            old = work.tile([P, COLS], F32)
            nc.vector.tensor_tensor(out=old[:], in0=kept["gate", FORGET][:], in1=kept["hyper_c_t"], op=ALU.mult)
            kept["old"] = old

        def new_part(group):
            if outside(group):
                return
            kept = kept_tiles[group]
            new = work.tile([P, COLS], F32)
            nc.vector.tensor_tensor(out=new[:], in0=kept["gate", INPUT][:], in1=kept["gate", CELL][:], op=ALU.mult)
            kept["new"] = new

        def transpose_rows(out, tiles):
            for t in range(TILES):
                for n, tile in enumerate(tiles):
                    nc.tensor.matmul(
                        out=out[:, t, :],
                        lhsT=tile[:, t * P : (t + 1) * P],
                        rhs=ident_f32[:],
                        start=n == 0,
                        stop=n == len(tiles) - 1,
                        is_transpose=True,
                    )

        def transpose_back(cell_group, gate_group):
            if not outside(cell_group) and cell_group >= N_GROUPS - LATE_GROUPS:
                late = psum_v.tile([P, 2, TILES, UNITS], F32, tag="v")
                kept = kept_tiles[cell_group]
                transpose_rows(late[:, 1, :, :], [kept["gate", OUTPUT]])
                transpose_rows(late[:, 0, :, :], [kept["old"], kept["new"]])
                kept["raw_c"] = late[:, 0, :, :]
                kept["gate_o_rows"] = late[:, 1, :, :]
            has_cell = 0 <= cell_group < N_GROUPS - LATE_GROUPS
            has_gate = 0 <= gate_group < N_GROUPS - LATE_GROUPS
            if not has_cell and not has_gate:
                return
            back = psum_back.tile([P, 2, TILES, UNITS], F32, tag="back")
            if has_gate:
                transpose_rows(back[:, 1, :, :], [kept_tiles[gate_group]["gate", OUTPUT]])
                kept_tiles[gate_group]["gate_o_rows"] = back[:, 1, :, :]
            if has_cell:
                transpose_rows(back[:, 0, :, :], [kept_tiles[cell_group]["old"], kept_tiles[cell_group]["new"]])
                kept_tiles[cell_group]["raw_c"] = back[:, 0, :, :]

        def cell_moments(group):
            if outside(group):
                return
            moments = shared_tiles[group + CELL_LAG]["moments"]
            nc.vector.bn_stats(
                out=moments[:, GATE_STATS:ROUND_STATS, :].rearrange("p s m -> p (s m)"),
                in_=kept_tiles[group]["raw_c"].rearrange("p t j -> p j t"),
            )

        def cell_centre(group):
            if outside(group):
                return
            kept = kept_tiles[group]
            centred = work.tile([P, TILES, UNITS], F32, bufs=4)
            for t in range(TILES):
                nc.vector.scalar_tensor_tensor(
                    out=centred[:, t, :],
                    in0=kept["raw_c"][:, t, :],
                    scalar=shared_tiles[group + CELL_LAG]["moments"][:, GATE_STATS + t, 1:2],
                    in1=gamma_c_all,
                    op0=ALU.subtract,
                    op1=ALU.mult,
                )
            kept["centred"] = centred

        def cell_out(group):
            if outside(group):
                return
            kept = kept_tiles[group]
            new_c = work.tile([P, TILES, UNITS], F32, bufs=3)
            for t in range(TILES):
                nc.vector.scalar_tensor_tensor(
                    out=new_c[:, t, :],
                    in0=kept["centred"][:, t, :],
                    scalar=shared_tiles[group + CELL_LAG]["inv"][:, GATE_STATS + t : GATE_STATS + t + 1],
                    in1=beta_c_all,
                    op0=ALU.mult,
                    op1=ALU.add,
                )
            kept["new_c"] = new_c[:].rearrange("p t j -> p (t j)")
            nc.sync.dma_start(out=new_c_rows[:, group * COLS : (group + 1) * COLS], in_=kept["new_c"])

        def cell_tanh(group):
            if outside(group):
                return
            kept = kept_tiles[group]
            tanh_c = work.tile([P, COLS], F32)
            nc.scalar.activation(out=tanh_c[:], in_=kept["new_c"], func=ACT.Tanh)
            kept["tanh_c"] = tanh_c

        def hidden_out(group):
            if outside(group):
                return
            kept = kept_tiles[group]
            new_h = work.tile([P, COLS], F32, bufs=3)
            nc.vector.tensor_tensor(
                out=new_h[:], in0=kept["gate_o_rows"].rearrange("p t j -> p (t j)"), in1=kept["tanh_c"][:], op=ALU.mult
            )
            nc.sync.dma_start(out=new_h_rows[:, group * COLS : (group + 1) * COLS], in_=new_h[:])

        def head():
            wih_first = transpose_wih(0)
            transpose_u(0)
            quantise_wih(nc.vector.tensor_copy, 0, wih_first)
            copy_u(0)
            wih_second = transpose_wih(1)
            quantise(0)
            vector_columns()
            transpose_states(0)
            quantise_wih(nc.scalar.copy, 1, wih_second)
            mx_product(0, 0)
            copy_states(0)
            transpose_whh()
            transpose_u(1)
            mx_product(0, 1)
            add_bias(0, 0)
            copy_u(1)
            add_bias(0, 1, on_vector=True)
            quantise(1)

        with tc.manual_schedule():
            head()
            for i in range(0, N_GROUPS):
                if i == 1:
                    spread_cell_vectors()
                load(i + 4)
                new_moments(i)
                plain_product(i, 1)
                plain_product(i, 0)
                mx_product(i + 1, 0)
                activate(i - 3, 1)
                cell_moments(i - 4)
                new_part(i - 3)
                cell_centre(i - 4)
                if i > 0:
                    copy_u(i + 2)
                add_mx_product(i, 0)
                add_mx_product(i, 1)
                if i == 0:
                    transpose_u(2)
                    transpose_states(1)
                add_bias(i + 1, 0)
                if i == 0:
                    copy_u(2)
                    copy_states(1)
                cell_tanh(i - 6)
                gate_moments(i, 0)
                std_eps(i - 1)
                hidden_out(i - 6)
                gate_moments(i, 1, (0,))
                inv_std(i - 1)
                gate_moments(i, 1, (1,))
                roots(i)
                gate_shift(i - 1)
                transpose_normed(i - 2, 0)
                transpose_states(i + 2)
                normalise_on_vector(i - 1)
                activate(i - 2, 0)
                copy_states(i + 2)
                mx_product(i + 1, 1)
                quantise(i + 2)
                cell_out(i - 5)
                add_bias(i + 1, 1)
                normalise_on_scalar(i - 1)
                old_part(i - 2)
                transpose_back(i - 3, i - 5)
                transpose_normed(i - 2, 1)
                transpose_u(i + 3)
            end = N_GROUPS
            for r in range(end, end + CELL_LAG):
                new_moments(r)
            transpose_normed(end - 2, 0)
            activate(end - 3, 1)
            cell_tanh(end - 6)
            transpose_normed(end - 2, 1)
            cell_moments(end - 4)
            new_part(end - 3)
            activate(end - 2, 0)
            cell_centre(end - 4)
            activate(end - 2, 1)
            old_part(end - 2)
            std_eps(end - 1)
            hidden_out(end - 6)
            inv_std(end - 1)
            new_part(end - 2)
            gate_shift(end - 1)
            transpose_back(end - 3, end - 5)
            normalise_on_vector(end - 1)
            normalise_on_scalar(end - 1)
            roots(end)
            transpose_back(end - 2, -1)
            transpose_normed(end - 1, 0)
            transpose_normed(end - 1, 1)
            cell_moments(end - 3)
            roots(end + 1)
            cell_out(end - 5)
            cell_centre(end - 3)
            activate(end - 1, 0)
            activate(end - 1, 1)
            cell_tanh(end - 5)
            std_eps(end)
            cell_moments(end - 2)
            inv_std(end)
            roots(end + 2)
            old_part(end - 1)
            new_part(end - 1)
            cell_centre(end - 2)
            cell_out(end - 4)
            hidden_out(end - 5)
            cell_tanh(end - 4)
            transpose_back(end - 1, end - 4)
            std_eps(end + 1)
            cell_moments(end - 1)
            inv_std(end + 1)
            roots(end + 3)
            cell_centre(end - 1)
            cell_out(end - 3)
            cell_tanh(end - 3)
            std_eps(end + 2)
            hidden_out(end - 4)
            inv_std(end + 2)
            hidden_out(end - 3)
            cell_out(end - 2)
            cell_tanh(end - 2)
            std_eps(end + 3)
            inv_std(end + 3)
            cell_out(end - 1)
            cell_tanh(end - 1)
            hidden_out(end - 2)
            hidden_out(end - 1)
